import numpy as np
import ml_dtypes


def mxq(x, axis, fmt="e4m3"):
    dtype, down = {"e4m3": (ml_dtypes.float8_e4m3fn, 7), "e5m2": (ml_dtypes.float8_e5m2, 14)}[fmt]
    v = np.moveaxis(np.asarray(x, np.float32).astype(ml_dtypes.bfloat16).astype(np.float64), axis, -1)
    blocks = v.reshape(v.shape[:-1] + (-1, 32))
    amax = np.abs(blocks).max(-1, keepdims=True)
    byte = np.maximum(np.where(amax > 0, np.frexp(amax)[1] - 1 + 127, 0) - down, 1)
    scale = np.exp2(byte - 127.0)
    codes = (blocks / scale).astype(np.float32).astype(dtype).astype(np.float64)
    return np.moveaxis((codes * scale).reshape(v.shape), -1, axis)


WIDE = False


def mx_kscale(k):
    if not WIDE:
        return np.ones(k)
    levels = np.array([10, -10, 5, -5, 0])
    a = np.random.permutation(np.resize(levels, k // 512 * 4)).reshape(k // 512, 4)
    idx = np.arange(k)
    return np.exp2(a[idx // 512, idx % 128 // 32])


BF16 = ml_dtypes.bfloat16


def bf(x):
    return np.asarray(x, np.float32).astype(BF16)


def f64(x):
    return np.asarray(x).astype(np.float64)


B, E, S, H = 4, 1024, 512, 16
DH = E // H


def setup_inputs():
    s = mx_kscale(S)
    return {"x_proj": bf(np.random.standard_normal((B, S, E)) * s[None, :, None]),
            "mix_mat": bf(np.random.standard_normal((H, S, S)) * np.sqrt(2.0 / S) / s[None, :, None]),
            "mix_b": bf(np.random.standard_normal((H, S)) * 0.2),
            "out_w": bf(np.random.standard_normal((E, E)) / np.sqrt(E)),
            "out_b": bf(np.random.standard_normal(E) * 0.2)}


def reference(x_proj, mix_mat, mix_b, out_w, out_b):
    p = f64(x_proj).reshape(B, S, H, DH).transpose(0, 2, 3, 1)
    idx = np.arange(S)
    keep = idx[None, :] >= idx[:, None]
    wm = np.where(keep[None], f64(mix_mat), 0.0)
    mixed = (mxq(p, 3, "e4m3") @ mxq(wm, 1, "e4m3")) + f64(mix_b)[None, :, None, :]
    y = mixed.transpose(0, 3, 1, 2).reshape(B, S, E)
    out = (mxq(y, 2, "e4m3") @ mxq(f64(out_w), 1, "e4m3").T) + f64(out_b)
    return out.transpose(0, 2, 1)

@@ -1,0 +1,265 @@
+from contextlib import ExitStack
+
+import concourse.mybir as mybir
+from concourse.masks import make_identity
+
+BF16 = mybir.dt.bfloat16
+F32 = mybir.dt.float32
+U32 = mybir.dt.uint32
+U8 = mybir.dt.uint8
+I32 = mybir.dt.int32
+FP8X4 = mybir.dt.float8_e4m3fn_x4
+ALU = mybir.AluOpType
+ACT = mybir.ActivationFunctionType
+
+P = 128
+B, S, E, H = 4, 512, 1024, 16
+FLOPS = 2 * B * E * S * S + 2 * B * S * E * E
+HC = 4
+NCK = H // HC
+PAIRW = 192
+HALF = 256
+ORDER = (1, 0)
+XV = 128
+
+
+def regroup(eng_copy, dst, src):
+    eng_copy(
+        out=dst.rearrange("p (c i) t -> p c t i", i=4),
+        in_=src.rearrange("p t (c i) -> p c t i", i=4),
+    )
+
+
+def tile_mixerblock_pa_kernel(tc, x_proj, mix_mat, mix_b, out_w, out_b, out):
+    nc = tc.nc
+    with ExitStack() as ctx:
+        keep = ctx.enter_context(tc.tile_pool(name="keep", bufs=1))
+        rot = ctx.enter_context(tc.tile_pool(name="rot", bufs=3))
+        xgp = ctx.enter_context(tc.tile_pool(name="xgp", bufs=2))
+        g1p = ctx.enter_context(tc.tile_pool(name="g1p", bufs=2))
+        ogp = ctx.enter_context(tc.tile_pool(name="ogp", bufs=2))
+        mgp = ctx.enter_context(tc.tile_pool(name="mgp", bufs=3))
+        otp = ctx.enter_context(tc.tile_pool(name="otp", bufs=4))
+        ps1p = ctx.enter_context(tc.psum_pool(name="ps1p", bufs=3))
+        ps2p = ctx.enter_context(tc.psum_pool(name="ps2p", bufs=3))
+        ptp = ctx.enter_context(tc.psum_pool(name="ptp", bufs=2))
+
+        xraw = {}
+        owraw = {}
+        xc = [keep.tile([P, 8 * PAIRW], U32, name="xc%d" % b, align_bytes=64) for b in range(B)]
+        xs = [keep.tile([P, 8 * PAIRW], U8, name="xs%d" % b, align_bytes=64) for b in range(B)]
+        wraw = [keep.tile([P, HC, 4, S], BF16, name="wraw%d" % k) for k in range(NCK)]
+        g0 = [keep.tile([P, 2, HALF, 4], BF16, name="g0_%d" % k, align_bytes=64) for k in range(2)]
+        wc = keep.tile([P, 2, H * HALF], U32, name="wc", align_bytes=64)
+        ws = keep.tile([P, 2, H * HALF], U8, name="ws", align_bytes=64)
+        oc = keep.tile([P, 2, E], U32, name="oc", align_bytes=64)
+        osc = keep.tile([P, 2, E], U8, name="osc", align_bytes=64)
+        mc = keep.tile([P, B, 2 * HALF], U32, name="mc", align_bytes=64)
+        ms = keep.tile([P, B, 2 * HALF], U8, name="ms", align_bytes=64)
+        bT = keep.tile([P, 8, S], BF16, name="bT")
+        ident = keep.tile([P, P], BF16, name="ident")
+        ones = keep.tile([P, P], F32, name="ones")
+        mask = keep.tile([P, P], BF16, name="mask")
+        obt = keep.tile([P, P], BF16, name="obt")
+        outb = keep.tile([P, 8], F32, name="outb")
+
+        def load_x(b):
+            xraw[b] = rot.tile([P, 4, E], BF16, name="xraw", tag="rot")
+            nc.sync.dma_start(out=xraw[b][:], in_=x_proj[b].rearrange("(j p) c -> p j c", p=P))
+
+        def load_ow(q):
+            owraw[q] = rot.tile([P, 4, E], BF16, name="owraw", tag="rot")
+            nc.sync.dma_start(
+                out=owraw[q][:], in_=out_w[512 * q:512 * (q + 1), :].rearrange("(ob p) c -> p ob c", p=P))
+
+        def load_w(k):
+            for j in range(4):
+                nc.sync.dma_start(
+                    out=wraw[k][:, :, j, P * j:S],
+                    in_=mix_mat[HC * k:HC * (k + 1), P * j:P * (j + 1), P * j:S].rearrange("h p s -> p h s"),
+                )
+
+        nc.gpsimd.memset(ones[:], 1.0)
+        nc.gpsimd.affine_select(
+            out=ones[:], in_=ones[:], pattern=[[1, P]], compare_op=ALU.is_ge,
+            fill=0.0, base=0, channel_multiplier=-1,
+        )
+        for k in range(NCK):
+            nc.gpsimd.memset(wraw[k][:, :, 3, 2 * P:3 * P], 0.0)
+        make_identity(nc, ident[:])
+        nc.gpsimd.memset(obt[:], 0.0)
+        for k in range(NCK):
+            nc.gpsimd.memset(wraw[k][:, :, 1, 0:P], 0.0)
+        for k in range(2):
+            nc.gpsimd.memset(g0[k][:], 0.0)
+        for b in range(B):
+            nc.vector.memset(
+                xc[b][:].bitcast(I32).rearrange("p (i w) -> p i w", w=PAIRW)[:, :, 64:128], 0)
+            nc.vector.memset(
+                xs[b][:].bitcast(I32).rearrange("p (i w) -> p i w", w=PAIRW // 4)[:, :, 16:32], 0)
+        nc.vector.tensor_copy(out=mask[:], in_=ones[:])
+
+        load_x(0)
+        load_w(0)
+        load_w(1)
+        load_x(1)
+        for h2 in range(2):
+            nc.sync.dma_start(
+                out=bT[64 * h2:64 * (h2 + 1), :, :],
+                in_=mix_b.rearrange("(i two) s -> two i s", two=2)[h2].partition_broadcast(64))
+        load_x(2)
+        load_w(2)
+        load_w(3)
+        nc.sync.dma_start(out=obt[0:8, :], in_=out_b.rearrange("(r c) -> r c", c=P))
+
+        def prep_x(b):
+            for ch in range(2):
+                xg = xgp.tile([P, 512, 4], BF16, name="xg", align_bytes=64)
+                c_lo = 512 * ch
+                regroup(nc.vector.tensor_copy, xg[:, 0:XV, :], xraw[b][:, :, c_lo:c_lo + XV])
+                regroup(nc.scalar.copy, xg[:, XV:512, :], xraw[b][:, :, c_lo + XV:c_lo + 512])
+                flat = xg[:].rearrange("p c t -> p (c t)")
+                w_lo = PAIRW * 4 * ch
+                spans = [(0, 64, w_lo)]
+                spans.extend((P * i + 64, P * i + 192, w_lo + PAIRW * i + P) for i in range(3))
+                spans.append((448, 512, w_lo + PAIRW * 3 + P))
+                for c0, c1, w0 in spans:
+                    nc.vector.quantize_mx(
+                        out=xc[b][:, w0:w0 + c1 - c0].bitcast(FP8X4),
+                        scales=xs[b][:, w0:w0 + c1 - c0],
+                        in_=flat[:, 4 * c0:4 * c1],
+                    )
+
+        def mask_w(k):
+            for j in range(4):
+                d = wraw[k][:, :, j, P * j:P * (j + 1)]
+                nc.vector.tensor_tensor(
+                    out=d, in0=d, in1=mask[:].unsqueeze(1).to_broadcast([P, HC, P]), op=ALU.mult)
+
+        def prep_w(k, half):
+            for q in range(2):
+                if half == 1:
+                    g = g1p.tile([P, 2, HALF, 4], BF16, name="g1", align_bytes=64)
+                    nslot = 4
+                else:
+                    g = g0[q]
+                    nslot = 2
+                for hh in range(2):
+                    eng = nc.vector.tensor_copy if (hh == 0 and half == 1) else nc.scalar.copy
+                    regroup(eng, g[:, hh, :, 0:nslot],
+                            wraw[k][:, 2 * q + hh, 0:nslot, HALF * half:HALF * (half + 1)])
+                w0 = (k * HC + 2 * q) * HALF
+                nc.vector.quantize_mx(
+                    out=wc[:, half, w0:w0 + 2 * HALF].bitcast(FP8X4),
+                    scales=ws[:, half, w0:w0 + 2 * HALF],
+                    in_=g[:].rearrange("p h s t -> p (h s t)"),
+                )
+
+        def prep_ow(g, obp):
+            pt = ptp.tile([P, 2, 4, P], BF16, name="pt")
+            for u in range(2):
+                for j in range(4):
+                    c0 = 512 * g + P * j
+                    nc.tensor.transpose(pt[:, u, j, :], owraw[obp // 2][:, 2 * (obp % 2) + u, c0:c0 + P], ident[:])
+            og = ogp.tile([P, 2, P, 4], BF16, name="og", align_bytes=64)
+            nc.scalar.copy(out=og[:], in_=pt[:].rearrange("p u j o -> p u o j"))
+            nc.vector.quantize_mx(
+                out=oc[:, g, 2 * P * obp:2 * P * (obp + 1)].bitcast(FP8X4),
+                scales=osc[:, g, 2 * P * obp:2 * P * (obp + 1)],
+                in_=og[:].rearrange("p u o j -> p (u o j)"),
+            )
+
+        def prep_outb():
+            pb = ptp.tile([P, P], BF16, name="pt")
+            nc.tensor.transpose(pb[:], obt[:], ident[:])
+            nc.vector.tensor_copy(out=outb[:], in_=pb[:, 0:8])
+
+        def stage1(half, b, g):
+            mg = mgp.tile([P, HALF, 4], BF16, name="mg", align_bytes=64)
+            for jl in range(2):
+                s0 = HALF * half + P * jl
+                acc = ps1p.tile([P, 4, P], F32, name="acc1")
+                for j in range(4):
+                    i = 4 * g + j
+                    for h2 in range(2):
+                        x0 = PAIRW * i + 64 * h2
+                        w0 = (2 * i + h2) * HALF + P * jl
+                        nc.tensor.matmul_mx(
+                            out=acc[:, j, :],
+                            lhsT=xc[b][:, x0:x0 + P].bitcast(FP8X4),
+                            lhsT_scale=xs[b][:, x0:x0 + P],
+                            rhs=wc[:, half, w0:w0 + P].bitcast(FP8X4),
+                            rhs_scale=ws[:, half, w0:w0 + P],
+                            start=(h2 == 0),
+                            stop=(h2 == 1),
+                        )
+                nc.vector.tensor_tensor(
+                    out=mg[:, P * jl:P * (jl + 1), :],
+                    in0=acc[:].rearrange("p j s -> p s j"),
+                    in1=bT[:, 4 * g:4 * g + 4, s0:s0 + P].rearrange("p j s -> p s j"),
+                    op=ALU.add,
+                )
+
+            nc.vector.quantize_mx(
+                out=mc[:, b, HALF * g:HALF * (g + 1)].bitcast(FP8X4),
+                scales=ms[:, b, HALF * g:HALF * (g + 1)],
+                in_=mg[:].rearrange("p s j -> p (s j)"),
+            )
+
+        def stage2(half, bp, ob):
+            acc = ps2p.tile([P, 2, HALF], F32, name="acc2")
+            for u in range(2):
+                for g in range(2):
+                    nc.tensor.matmul_mx(
+                        out=acc[:, u, :],
+                        lhsT=oc[:, g, P * ob:P * (ob + 1)].bitcast(FP8X4),
+                        lhsT_scale=osc[:, g, P * ob:P * (ob + 1)],
+                        rhs=mc[:, 2 * bp + u, HALF * g:HALF * (g + 1)].bitcast(FP8X4),
+                        rhs_scale=ms[:, 2 * bp + u, HALF * g:HALF * (g + 1)],
+                        start=(g == 0),
+                        stop=(g == 1),
+                    )
+            ot = otp.tile([P, 2, HALF], F32, name="ot")
+            nc.scalar.activation(out=ot[:], in_=acc[:], func=ACT.Identity, bias=outb[:, ob:ob + 1], scale=1.0)
+            nc.sync.dma_start(
+                out=out[2 * bp:2 * bp + 2, P * ob:P * (ob + 1), HALF * half:HALF * (half + 1)].rearrange("b p s -> p b s"),
+                in_=ot[:],
+            )
+
+        h_a, h_b = ORDER
+        prep_x(0)
+        load_x(3)
+        mask_w(0)
+        prep_w(0, h_a)
+        mask_w(1)
+        prep_w(1, h_a)
+        stage1(h_a, 0, 0)
+        prep_x(1)
+        load_ow(0)
+        stage1(h_a, 1, 0)
+        prep_x(2)
+        load_ow(1)
+        stage1(h_a, 2, 0)
+        prep_x(3)
+        stage1(h_a, 3, 0)
+        mask_w(2)
+        prep_w(2, h_a)
+        mask_w(3)
+        prep_w(3, h_a)
+        for b in range(B):
+            stage1(h_a, b, 1)
+        prep_outb()
+        for g in range(2):
+            for obp in range(4):
+                prep_ow(g, obp)
+        for bp in range(2):
+            for ob in range(8):
+                stage2(h_a, bp, ob)
+            prep_w(2 * bp, h_b)
+            prep_w(2 * bp + 1, h_b)
+        for b in range(B):
+            stage1(h_b, b, 0)
+            stage1(h_b, b, 1)
+        for bp in range(2):
+            for ob in range(8):
+                stage2(h_b, bp, ob)

@@ -20,7 +20,6 @@ NCK = H // HC
 PAIRW = 192
 HALF = 256
 ORDER = (1, 0)
-XV = 128
 
 
 def regroup(eng_copy, dst, src):
@@ -36,26 +35,24 @@ def tile_mixerblock_pa_kernel(tc, x_proj, mix_mat, mix_b, out_w, out_b, out):
         keep = ctx.enter_context(tc.tile_pool(name="keep", bufs=1))
         rot = ctx.enter_context(tc.tile_pool(name="rot", bufs=3))
         xgp = ctx.enter_context(tc.tile_pool(name="xgp", bufs=2))
-        g1p = ctx.enter_context(tc.tile_pool(name="g1p", bufs=2))
+        g1p = ctx.enter_context(tc.tile_pool(name="g1p", bufs=3))
         ogp = ctx.enter_context(tc.tile_pool(name="ogp", bufs=2))
         mgp = ctx.enter_context(tc.tile_pool(name="mgp", bufs=3))
-        otp = ctx.enter_context(tc.tile_pool(name="otp", bufs=4))
-        ps1p = ctx.enter_context(tc.psum_pool(name="ps1p", bufs=3))
-        ps2p = ctx.enter_context(tc.psum_pool(name="ps2p", bufs=3))
-        ptp = ctx.enter_context(tc.psum_pool(name="ptp", bufs=2))
+        ps1p = ctx.enter_context(tc.psum_pool(name="ps1p", bufs=4))
+        ps2p = ctx.enter_context(tc.psum_pool(name="ps2p", bufs=4))
 
         xraw = {}
         owraw = {}
         xc = [keep.tile([P, 8 * PAIRW], U32, name="xc%d" % b, align_bytes=64) for b in range(B)]
         xs = [keep.tile([P, 8 * PAIRW], U8, name="xs%d" % b, align_bytes=64) for b in range(B)]
         wraw = [keep.tile([P, HC, 4, S], BF16, name="wraw%d" % k) for k in range(NCK)]
-        g0 = [keep.tile([P, 2, HALF, 4], BF16, name="g0_%d" % k, align_bytes=64) for k in range(2)]
+        g0 = [keep.tile([P, HALF, 4], BF16, name="g0_%d" % k, align_bytes=64) for k in range(2)]
         wc = keep.tile([P, 2, H * HALF], U32, name="wc", align_bytes=64)
         ws = keep.tile([P, 2, H * HALF], U8, name="ws", align_bytes=64)
         oc = keep.tile([P, 2, E], U32, name="oc", align_bytes=64)
         osc = keep.tile([P, 2, E], U8, name="osc", align_bytes=64)
-        mc = keep.tile([P, B, 2 * HALF], U32, name="mc", align_bytes=64)
-        ms = keep.tile([P, B, 2 * HALF], U8, name="ms", align_bytes=64)
+        mc = keep.tile([P, 2, B, 2 * HALF], U32, name="mc", align_bytes=64)
+        ms = keep.tile([P, 2, B, 2 * HALF], U8, name="ms", align_bytes=64)
         bT = keep.tile([P, 8, S], BF16, name="bT")
         ident = keep.tile([P, P], BF16, name="ident")
         ones = keep.tile([P, P], F32, name="ones")
@@ -103,82 +100,95 @@ def tile_mixerblock_pa_kernel(tc, x_proj, mix_mat, mix_b, out_w, out_b, out):
         load_w(0)
         load_w(1)
         load_x(1)
-        for h2 in range(2):
-            nc.sync.dma_start(
-                out=bT[64 * h2:64 * (h2 + 1), :, :],
-                in_=mix_b.rearrange("(i two) s -> two i s", two=2)[h2].partition_broadcast(64))
         load_x(2)
+        nc.sync.dma_start(
+            out=bT[0:64, :, :], in_=mix_b.rearrange("(i two) s -> two i s", two=2)[0].partition_broadcast(64))
+        nc.scalar.dma_start(
+            out=bT[64:128, :, :], in_=mix_b.rearrange("(i two) s -> two i s", two=2)[1].partition_broadcast(64))
         load_w(2)
         load_w(3)
         nc.sync.dma_start(out=obt[0:8, :], in_=out_b.rearrange("(r c) -> r c", c=P))
 
-        def prep_x(b):
-            for ch in range(2):
-                xg = xgp.tile([P, 512, 4], BF16, name="xg", align_bytes=64)
-                c_lo = 512 * ch
-                regroup(nc.vector.tensor_copy, xg[:, 0:XV, :], xraw[b][:, :, c_lo:c_lo + XV])
-                regroup(nc.scalar.copy, xg[:, XV:512, :], xraw[b][:, :, c_lo + XV:c_lo + 512])
-                flat = xg[:].rearrange("p c t -> p (c t)")
-                w_lo = PAIRW * 4 * ch
-                spans = [(0, 64, w_lo)]
-                spans.extend((P * i + 64, P * i + 192, w_lo + PAIRW * i + P) for i in range(3))
-                spans.append((448, 512, w_lo + PAIRW * 3 + P))
-                for c0, c1, w0 in spans:
-                    nc.vector.quantize_mx(
-                        out=xc[b][:, w0:w0 + c1 - c0].bitcast(FP8X4),
-                        scales=xs[b][:, w0:w0 + c1 - c0],
-                        in_=flat[:, 4 * c0:4 * c1],
-                    )
+        xg_of = {}
 
-        def mask_w(k):
-            for j in range(4):
+        def x_regroup(b, ch):
+            xg = xgp.tile([P, 512, 4], BF16, name="xg", align_bytes=64)
+            xg_of[(b, ch)] = xg
+            c_lo = 512 * ch
+            for q in range(2):
+                eng = nc.vector.tensor_copy if (b == 0 and q == 0) else nc.scalar.copy
+                regroup(eng, xg[:, 256 * q:256 * (q + 1), :],
+                        xraw[b][:, :, c_lo + 256 * q:c_lo + 256 * (q + 1)])
+
+        def x_quant(b, ch):
+            flat = xg_of[(b, ch)][:].rearrange("p c t -> p (c t)")
+            w_lo = PAIRW * 4 * ch
+            spans = [(0, 64, w_lo)]
+            spans.extend((P * i + 64, P * i + 192, w_lo + PAIRW * i + P) for i in range(3))
+            spans.append((448, 512, w_lo + PAIRW * 3 + P))
+            for c0, c1, w0 in spans:
+                nc.vector.quantize_mx(
+                    out=xc[b][:, w0:w0 + c1 - c0].bitcast(FP8X4),
+                    scales=xs[b][:, w0:w0 + c1 - c0],
+                    in_=flat[:, 4 * c0:4 * c1],
+                )
+
+        def w_mask(k, slots):
+            for j in slots:
                 d = wraw[k][:, :, j, P * j:P * (j + 1)]
                 nc.vector.tensor_tensor(
                     out=d, in0=d, in1=mask[:].unsqueeze(1).to_broadcast([P, HC, P]), op=ALU.mult)
 
-        def prep_w(k, half):
-            for q in range(2):
-                if half == 1:
-                    g = g1p.tile([P, 2, HALF, 4], BF16, name="g1", align_bytes=64)
-                    nslot = 4
-                else:
-                    g = g0[q]
-                    nslot = 2
-                for hh in range(2):
-                    eng = nc.vector.tensor_copy if (hh == 0 and half == 1) else nc.scalar.copy
-                    regroup(eng, g[:, hh, :, 0:nslot],
-                            wraw[k][:, 2 * q + hh, 0:nslot, HALF * half:HALF * (half + 1)])
-                w0 = (k * HC + 2 * q) * HALF
-                nc.vector.quantize_mx(
-                    out=wc[:, half, w0:w0 + 2 * HALF].bitcast(FP8X4),
-                    scales=ws[:, half, w0:w0 + 2 * HALF],
-                    in_=g[:].rearrange("p h s t -> p (h s t)"),
-                )
+        g_of = {}
 
-        def prep_ow(g, obp):
-            pt = ptp.tile([P, 2, 4, P], BF16, name="pt")
+        def w_prep(h, half):
+            if half == 1:
+                g = g1p.tile([P, HALF, 4], BF16, name="g1", align_bytes=64)
+                eng = nc.vector.tensor_copy if h % 4 == 0 else nc.scalar.copy
+                regroup(eng, g[:], wraw[h // HC][:, h % HC, :, HALF:2 * HALF])
+            else:
+                g = g0[h % 2]
+                regroup(nc.vector.tensor_copy, g[:, :, 0:2], wraw[h // HC][:, h % HC, 0:2, 0:HALF])
+            nc.vector.quantize_mx(
+                out=wc[:, half, h * HALF:(h + 1) * HALF].bitcast(FP8X4),
+                scales=ws[:, half, h * HALF:(h + 1) * HALF],
+                in_=g[:].rearrange("p s t -> p (s t)"),
+            )
+
+        pt_of = {}
+        og_of = {}
+
+        def ow_transpose(obp, g):
+            pt = ps2p.tile([P, 2, 4, P], BF16, name="pt", tag="ps2")
+            pt_of[(obp, g)] = pt
             for u in range(2):
                 for j in range(4):
                     c0 = 512 * g + P * j
                     nc.tensor.transpose(pt[:, u, j, :], owraw[obp // 2][:, 2 * (obp % 2) + u, c0:c0 + P], ident[:])
+
+        def ow_exit(obp, g):
             og = ogp.tile([P, 2, P, 4], BF16, name="og", align_bytes=64)
-            nc.scalar.copy(out=og[:], in_=pt[:].rearrange("p u j o -> p u o j"))
+            og_of[(obp, g)] = og
+            nc.scalar.copy(out=og[:], in_=pt_of[(obp, g)][:].rearrange("p u j o -> p u o j"))
+
+        def ow_quant(obp, g):
             nc.vector.quantize_mx(
                 out=oc[:, g, 2 * P * obp:2 * P * (obp + 1)].bitcast(FP8X4),
                 scales=osc[:, g, 2 * P * obp:2 * P * (obp + 1)],
-                in_=og[:].rearrange("p u o j -> p (u o j)"),
+                in_=og_of[(obp, g)][:].rearrange("p u o j -> p (u o j)"),
             )
 
         def prep_outb():
-            pb = ptp.tile([P, P], BF16, name="pt")
+            pb = ps2p.tile([P, P], BF16, name="pb", tag="ps2")
             nc.tensor.transpose(pb[:], obt[:], ident[:])
             nc.vector.tensor_copy(out=outb[:], in_=pb[:, 0:8])
 
-        def stage1(half, b, g):
-            mg = mgp.tile([P, HALF, 4], BF16, name="mg", align_bytes=64)
+        acc1_of = {}
+
+        def mix_mm(half, b, g):
             for jl in range(2):
-                s0 = HALF * half + P * jl
                 acc = ps1p.tile([P, 4, P], F32, name="acc1")
+                acc1_of[(half, b, g, jl)] = acc
                 for j in range(4):
                     i = 4 * g + j
                     for h2 in range(2):
@@ -193,73 +203,111 @@ def tile_mixerblock_pa_kernel(tc, x_proj, mix_mat, mix_b, out_w, out_b, out):
                             start=(h2 == 0),
                             stop=(h2 == 1),
                         )
+
+        def mix_exit(half, b, g):
+            mg = mgp.tile([P, HALF, 4], BF16, name="mg", align_bytes=64)
+            for jl in range(2):
+                s0 = HALF * half + P * jl
                 nc.vector.tensor_tensor(
                     out=mg[:, P * jl:P * (jl + 1), :],
-                    in0=acc[:].rearrange("p j s -> p s j"),
+                    in0=acc1_of[(half, b, g, jl)][:].rearrange("p j s -> p s j"),
                     in1=bT[:, 4 * g:4 * g + 4, s0:s0 + P].rearrange("p j s -> p s j"),
                     op=ALU.add,
                 )
-
             nc.vector.quantize_mx(
-                out=mc[:, b, HALF * g:HALF * (g + 1)].bitcast(FP8X4),
-                scales=ms[:, b, HALF * g:HALF * (g + 1)],
+                out=mc[:, half, b, HALF * g:HALF * (g + 1)].bitcast(FP8X4),
+                scales=ms[:, half, b, HALF * g:HALF * (g + 1)],
                 in_=mg[:].rearrange("p s j -> p (s j)"),
             )
 
-        def stage2(half, bp, ob):
-            acc = ps2p.tile([P, 2, HALF], F32, name="acc2")
+        acc2_of = {}
+
+        def out_mm(half, bp, ob):
+            acc = ps2p.tile([P, 2, HALF], F32, name="acc2", tag="ps2")
+            acc2_of[(half, bp, ob)] = acc
             for u in range(2):
                 for g in range(2):
                     nc.tensor.matmul_mx(
                         out=acc[:, u, :],
                         lhsT=oc[:, g, P * ob:P * (ob + 1)].bitcast(FP8X4),
                         lhsT_scale=osc[:, g, P * ob:P * (ob + 1)],
-                        rhs=mc[:, 2 * bp + u, HALF * g:HALF * (g + 1)].bitcast(FP8X4),
-                        rhs_scale=ms[:, 2 * bp + u, HALF * g:HALF * (g + 1)],
+                        rhs=mc[:, half, 2 * bp + u, HALF * g:HALF * (g + 1)].bitcast(FP8X4),
+                        rhs_scale=ms[:, half, 2 * bp + u, HALF * g:HALF * (g + 1)],
                         start=(g == 0),
                         stop=(g == 1),
                     )
-            ot = otp.tile([P, 2, HALF], F32, name="ot")
-            nc.scalar.activation(out=ot[:], in_=acc[:], func=ACT.Identity, bias=outb[:, ob:ob + 1], scale=1.0)
+
+        ot_of = {}
+
+        def out_exit(half, bp, ob, on_vector=False):
+            if ob % 4 == 0:
+                ot_of[0] = rot.tile([P, 4, 2, HALF], F32, name="ot4", tag="rot")
+            ot = ot_of[0][:, ob % 4]
+            acc = acc2_of[(half, bp, ob)]
+            if on_vector:
+                nc.vector.tensor_scalar(out=ot, in0=acc[:], scalar1=outb[:, ob:ob + 1], scalar2=None, op0=ALU.add)
+            else:
+                nc.scalar.activation(out=ot, in_=acc[:], func=ACT.Identity, bias=outb[:, ob:ob + 1], scale=1.0)
             nc.sync.dma_start(
                 out=out[2 * bp:2 * bp + 2, P * ob:P * (ob + 1), HALF * half:HALF * (half + 1)].rearrange("b p s -> p b s"),
-                in_=ot[:],
+                in_=ot,
             )
 
-        h_a, h_b = ORDER
-        prep_x(0)
+        def x_prep(b):
+            for ch in range(2):
+                x_regroup(b, ch)
+                x_quant(b, ch)
+
+        def mix(half, b, g):
+            mix_mm(half, b, g)
+            mix_exit(half, b, g)
+
+        def project(half, bp, both):
+            for ob in range(8):
+                out_mm(half, bp, ob)
+                out_exit(half, bp, ob, on_vector=(both and ob % 2 == 1))
+
+        x_prep(0)
         load_x(3)
-        mask_w(0)
-        prep_w(0, h_a)
-        mask_w(1)
-        prep_w(1, h_a)
-        stage1(h_a, 0, 0)
-        prep_x(1)
+        for k in range(2):
+            w_mask(k, (2, 3))
+            for h in range(HC * k, HC * (k + 1)):
+                w_prep(h, 1)
+        mix(1, 0, 0)
+        x_prep(1)
         load_ow(0)
-        stage1(h_a, 1, 0)
-        prep_x(2)
+        mix(1, 1, 0)
+        x_prep(2)
         load_ow(1)
-        stage1(h_a, 2, 0)
-        prep_x(3)
-        stage1(h_a, 3, 0)
-        mask_w(2)
-        prep_w(2, h_a)
-        mask_w(3)
-        prep_w(3, h_a)
-        for b in range(B):
-            stage1(h_a, b, 1)
+        mix(1, 2, 0)
+        for k in range(2, 4):
+            w_mask(k, (2, 3))
+            for h in range(HC * k, HC * (k + 1)):
+                w_prep(h, 1)
+        mix(1, 0, 1)
+        mix(1, 1, 1)
         prep_outb()
-        for g in range(2):
-            for obp in range(4):
-                prep_ow(g, obp)
-        for bp in range(2):
-            for ob in range(8):
-                stage2(h_a, bp, ob)
-            prep_w(2 * bp, h_b)
-            prep_w(2 * bp + 1, h_b)
-        for b in range(B):
-            stage1(h_b, b, 0)
-            stage1(h_b, b, 1)
-        for bp in range(2):
-            for ob in range(8):
-                stage2(h_b, bp, ob)
+        for obp in range(4):
+            for g in range(2):
+                ow_transpose(obp, g)
+                ow_exit(obp, g)
+                ow_quant(obp, g)
+        project(1, 0, False)
+        x_prep(3)
+        mix(1, 3, 0)
+        mix(1, 2, 1)
+        mix(1, 3, 1)
+        project(1, 1, False)
+        for k in range(4):
+            w_mask(k, (0, 1))
+            for h in range(HC * k, HC * (k + 1)):
+                w_prep(h, 0)
+            if k == 1:
+                for b in range(B):
+                    mix(0, b, 0)
+        mix(0, 0, 1)
+        mix(0, 1, 1)
+        project(0, 0, False)
+        mix(0, 2, 1)
+        mix(0, 3, 1)
+        project(0, 1, True)

@@ -46,7 +46,7 @@ def tile_mixerblock_pa_kernel(tc, x_proj, mix_mat, mix_b, out_w, out_b, out):
         xc = [keep.tile([P, 8 * PAIRW], U32, name="xc%d" % b, align_bytes=64) for b in range(B)]
         xs = [keep.tile([P, 8 * PAIRW], U8, name="xs%d" % b, align_bytes=64) for b in range(B)]
         wraw = [keep.tile([P, HC, 4, S], BF16, name="wraw%d" % k) for k in range(NCK)]
-        g0 = [keep.tile([P, HALF, 4], BF16, name="g0_%d" % k, align_bytes=64) for k in range(2)]
+        g0 = [keep.tile([P, HALF, 4], BF16, name="g0_%d" % k, align_bytes=64) for k in range(3)]
         wc = keep.tile([P, 2, H * HALF], U32, name="wc", align_bytes=64)
         ws = keep.tile([P, 2, H * HALF], U8, name="ws", align_bytes=64)
         oc = keep.tile([P, 2, E], U32, name="oc", align_bytes=64)
@@ -87,7 +87,7 @@ def tile_mixerblock_pa_kernel(tc, x_proj, mix_mat, mix_b, out_w, out_b, out):
         nc.gpsimd.memset(obt[:], 0.0)
         for k in range(NCK):
             nc.gpsimd.memset(wraw[k][:, :, 1, 0:P], 0.0)
-        for k in range(2):
+        for k in range(3):
             nc.gpsimd.memset(g0[k][:], 0.0)
         for b in range(B):
             nc.vector.memset(
@@ -141,19 +141,31 @@ def tile_mixerblock_pa_kernel(tc, x_proj, mix_mat, mix_b, out_w, out_b, out):
 
         g_of = {}
 
+        late_w = []
+        late_m = []
+
+        def flush(late):
+            for call in late:
+                call()
+            late[0:len(late)] = []
+
+        def defer(late, call):
+            flush(late)
+            late.append(call)
+
         def w_prep(h, half):
             if half == 1:
                 g = g1p.tile([P, HALF, 4], BF16, name="g1", align_bytes=64)
                 eng = nc.vector.tensor_copy if h % 4 == 0 else nc.scalar.copy
                 regroup(eng, g[:], wraw[h // HC][:, h % HC, :, HALF:2 * HALF])
             else:
-                g = g0[h % 2]
+                g = g0[h % 3]
                 regroup(nc.vector.tensor_copy, g[:, :, 0:2], wraw[h // HC][:, h % HC, 0:2, 0:HALF])
-            nc.vector.quantize_mx(
+            defer(late_w, lambda: nc.vector.quantize_mx(
                 out=wc[:, half, h * HALF:(h + 1) * HALF].bitcast(FP8X4),
                 scales=ws[:, half, h * HALF:(h + 1) * HALF],
                 in_=g[:].rearrange("p s t -> p (s t)"),
-            )
+            ))
 
         pt_of = {}
         og_of = {}
@@ -186,6 +198,7 @@ def tile_mixerblock_pa_kernel(tc, x_proj, mix_mat, mix_b, out_w, out_b, out):
         acc1_of = {}
 
         def mix_mm(half, b, g):
+            flush(late_w)
             for jl in range(2):
                 acc = ps1p.tile([P, 4, P], F32, name="acc1")
                 acc1_of[(half, b, g, jl)] = acc
@@ -214,43 +227,49 @@ def tile_mixerblock_pa_kernel(tc, x_proj, mix_mat, mix_b, out_w, out_b, out):
                     in1=bT[:, 4 * g:4 * g + 4, s0:s0 + P].rearrange("p j s -> p s j"),
                     op=ALU.add,
                 )
-            nc.vector.quantize_mx(
+                if jl == 0:
+                    flush(late_m)
+            late_m.append(lambda: nc.vector.quantize_mx(
                 out=mc[:, half, b, HALF * g:HALF * (g + 1)].bitcast(FP8X4),
                 scales=ms[:, half, b, HALF * g:HALF * (g + 1)],
                 in_=mg[:].rearrange("p s j -> p (s j)"),
-            )
+            ))
 
         acc2_of = {}
 
-        def out_mm(half, bp, ob):
+        def out_mm(half, b, obp):
+            flush(late_m)
             acc = ps2p.tile([P, 2, HALF], F32, name="acc2", tag="ps2")
-            acc2_of[(half, bp, ob)] = acc
+            acc2_of[(half, b, obp)] = acc
             for u in range(2):
+                ob = 2 * obp + u
                 for g in range(2):
                     nc.tensor.matmul_mx(
                         out=acc[:, u, :],
                         lhsT=oc[:, g, P * ob:P * (ob + 1)].bitcast(FP8X4),
                         lhsT_scale=osc[:, g, P * ob:P * (ob + 1)],
-                        rhs=mc[:, half, 2 * bp + u, HALF * g:HALF * (g + 1)].bitcast(FP8X4),
-                        rhs_scale=ms[:, half, 2 * bp + u, HALF * g:HALF * (g + 1)],
+                        rhs=mc[:, half, b, HALF * g:HALF * (g + 1)].bitcast(FP8X4),
+                        rhs_scale=ms[:, half, b, HALF * g:HALF * (g + 1)],
                         start=(g == 0),
                         stop=(g == 1),
                     )
 
         ot_of = {}
 
-        def out_exit(half, bp, ob, on_vector=False):
-            if ob % 4 == 0:
-                ot_of[0] = rot.tile([P, 4, 2, HALF], F32, name="ot4", tag="rot")
-            ot = ot_of[0][:, ob % 4]
-            acc = acc2_of[(half, bp, ob)]
-            if on_vector:
-                nc.vector.tensor_scalar(out=ot, in0=acc[:], scalar1=outb[:, ob:ob + 1], scalar2=None, op0=ALU.add)
-            else:
-                nc.scalar.activation(out=ot, in_=acc[:], func=ACT.Identity, bias=outb[:, ob:ob + 1], scale=1.0)
+        def out_exit(half, b, obp, both):
+            if obp == 0:
+                ot_of[0] = rot.tile([P, 8, HALF], F32, name="ot8", tag="rot")
+            acc = acc2_of[(half, b, obp)]
+            for u in range(2):
+                ob = 2 * obp + u
+                ot = ot_of[0][:, ob, :]
+                if both and u == 1:
+                    nc.vector.tensor_scalar(out=ot, in0=acc[:, u, :], scalar1=outb[:, ob:ob + 1], scalar2=None, op0=ALU.add)
+                else:
+                    nc.scalar.activation(out=ot, in_=acc[:, u, :], func=ACT.Identity, bias=outb[:, ob:ob + 1], scale=1.0)
             nc.sync.dma_start(
-                out=out[2 * bp:2 * bp + 2, P * ob:P * (ob + 1), HALF * half:HALF * (half + 1)].rearrange("b p s -> p b s"),
-                in_=ot,
+                out=out[b, 2 * P * obp:2 * P * (obp + 1), HALF * half:HALF * (half + 1)].rearrange("(u p) s -> p u s", p=P),
+                in_=ot_of[0][:, 2 * obp:2 * obp + 2, :],
             )
 
         def x_prep(b):
@@ -258,32 +277,35 @@ def tile_mixerblock_pa_kernel(tc, x_proj, mix_mat, mix_b, out_w, out_b, out):
                 x_regroup(b, ch)
                 x_quant(b, ch)
 
+        def w_chunk(k, half):
+            w_mask(k, (2, 3) if half == 1 else (0, 1))
+            for h in range(HC * k, HC * (k + 1)):
+                w_prep(h, half)
+
         def mix(half, b, g):
             mix_mm(half, b, g)
             mix_exit(half, b, g)
 
-        def project(half, bp, both):
-            for ob in range(8):
-                out_mm(half, bp, ob)
-                out_exit(half, bp, ob, on_vector=(both and ob % 2 == 1))
+        def project(half, b, both):
+            for obp in range(4):
+                out_mm(half, b, obp)
+                out_exit(half, b, obp, both)
 
         x_prep(0)
         load_x(3)
-        for k in range(2):
-            w_mask(k, (2, 3))
-            for h in range(HC * k, HC * (k + 1)):
-                w_prep(h, 1)
+        w_chunk(0, 1)
+        w_chunk(1, 1)
         mix(1, 0, 0)
+        w_chunk(0, 0)
+        w_chunk(1, 0)
         x_prep(1)
         load_ow(0)
         mix(1, 1, 0)
         x_prep(2)
         load_ow(1)
         mix(1, 2, 0)
-        for k in range(2, 4):
-            w_mask(k, (2, 3))
-            for h in range(HC * k, HC * (k + 1)):
-                w_prep(h, 1)
+        w_chunk(2, 1)
+        w_chunk(3, 1)
         mix(1, 0, 1)
         mix(1, 1, 1)
         prep_outb()
@@ -293,21 +315,17 @@ def tile_mixerblock_pa_kernel(tc, x_proj, mix_mat, mix_b, out_w, out_b, out):
                 ow_exit(obp, g)
                 ow_quant(obp, g)
         project(1, 0, False)
-        x_prep(3)
-        mix(1, 3, 0)
-        mix(1, 2, 1)
-        mix(1, 3, 1)
         project(1, 1, False)
-        for k in range(4):
-            w_mask(k, (0, 1))
-            for h in range(HC * k, HC * (k + 1)):
-                w_prep(h, 0)
-            if k == 1:
-                for b in range(B):
-                    mix(0, b, 0)
-        mix(0, 0, 1)
-        mix(0, 1, 1)
-        project(0, 0, False)
-        mix(0, 2, 1)
-        mix(0, 3, 1)
-        project(0, 1, True)
+        x_prep(3)
+        mix(1, 2, 1)
+        project(1, 2, False)
+        mix(1, 3, 0)
+        mix(1, 3, 1)
+        project(1, 3, False)
+        for b in range(B):
+            mix(0, b, 0)
+        w_chunk(2, 0)
+        w_chunk(3, 0)
+        for b in range(B):
+            mix(0, b, 1)
+            project(0, b, b == 3)

@@ -53,7 +53,9 @@ def tile_mixerblock_pa_kernel(tc, x_proj, mix_mat, mix_b, out_w, out_b, out):
         osc = keep.tile([P, 2, E], U8, name="osc", align_bytes=64)
         mc = keep.tile([P, 2, B, 2 * HALF], U32, name="mc", align_bytes=64)
         ms = keep.tile([P, 2, B, 2 * HALF], U8, name="ms", align_bytes=64)
-        bT = keep.tile([P, 8, S], BF16, name="bT")
+        bT = keep.tile([P, 2, 4, P, 4], BF16, name="bT")
+        mb = keep.tile([P, S], BF16, name="mb")
+        sel = keep.tile([P, 8, P], BF16, name="sel")
         ident = keep.tile([P, P], BF16, name="ident")
         ones = keep.tile([P, P], F32, name="ones")
         mask = keep.tile([P, P], BF16, name="mask")
@@ -76,6 +78,8 @@ def tile_mixerblock_pa_kernel(tc, x_proj, mix_mat, mix_b, out_w, out_b, out):
                     in_=mix_mat[HC * k:HC * (k + 1), P * j:P * (j + 1), P * j:S].rearrange("h p s -> p h s"),
                 )
 
+        nc.gpsimd.memset(mb[:], 0.0)
+        make_identity(nc, ident[:])
         nc.gpsimd.memset(ones[:], 1.0)
         nc.gpsimd.affine_select(
             out=ones[:], in_=ones[:], pattern=[[1, P]], compare_op=ALU.is_ge,
@@ -83,7 +87,6 @@ def tile_mixerblock_pa_kernel(tc, x_proj, mix_mat, mix_b, out_w, out_b, out):
         )
         for k in range(NCK):
             nc.gpsimd.memset(wraw[k][:, :, 3, 2 * P:3 * P], 0.0)
-        make_identity(nc, ident[:])
         nc.gpsimd.memset(obt[:], 0.0)
         for k in range(NCK):
             nc.gpsimd.memset(wraw[k][:, :, 1, 0:P], 0.0)
@@ -96,15 +99,12 @@ def tile_mixerblock_pa_kernel(tc, x_proj, mix_mat, mix_b, out_w, out_b, out):
                 xs[b][:].bitcast(I32).rearrange("p (i w) -> p i w", w=PAIRW // 4)[:, :, 16:32], 0)
         nc.vector.tensor_copy(out=mask[:], in_=ones[:])
 
+        nc.scalar.dma_start(out=mb[0:H, :], in_=mix_b)
         load_x(0)
         load_w(0)
         load_w(1)
         load_x(1)
         load_x(2)
-        nc.sync.dma_start(
-            out=bT[0:64, :, :], in_=mix_b.rearrange("(i two) s -> two i s", two=2)[0].partition_broadcast(64))
-        nc.scalar.dma_start(
-            out=bT[64:128, :, :], in_=mix_b.rearrange("(i two) s -> two i s", two=2)[1].partition_broadcast(64))
         load_w(2)
         load_w(3)
         nc.sync.dma_start(out=obt[0:8, :], in_=out_b.rearrange("(r c) -> r c", c=P))
@@ -190,6 +190,20 @@ def tile_mixerblock_pa_kernel(tc, x_proj, mix_mat, mix_b, out_w, out_b, out):
                 in_=og_of[(obp, g)][:].rearrange("p u o j -> p (u o j)"),
             )
 
+        def prep_bias():
+            pairs = ident[:, 0:H].rearrange("p (i two) -> p i two", two=2)
+            for h2 in range(2):
+                nc.vector.tensor_copy(out=sel[:, :, 64 * h2:64 * (h2 + 1)],
+                                      in_=pairs[:, :, h2:h2 + 1].to_broadcast([P, 8, 64]))
+            for g in range(2):
+                for sb in range(4):
+                    pbias = ps1p.tile([P, 4, P], F32, name="acc1")
+                    for j in range(4):
+                        nc.tensor.matmul(out=pbias[:, j, :], lhsT=sel[:, 4 * g + j, :], rhs=mb[:, P * sb:P * (sb + 1)],
+                                         start=True, stop=True)
+                    eng = nc.scalar.copy
+                    eng(out=bT[:, g, sb], in_=pbias[:].rearrange("p j s -> p s j"))
+
         def prep_outb():
             pb = ps2p.tile([P, P], BF16, name="pb", tag="ps2")
             nc.tensor.transpose(pb[:], obt[:], ident[:])
@@ -224,7 +238,7 @@ def tile_mixerblock_pa_kernel(tc, x_proj, mix_mat, mix_b, out_w, out_b, out):
                 nc.vector.tensor_tensor(
                     out=mg[:, P * jl:P * (jl + 1), :],
                     in0=acc1_of[(half, b, g, jl)][:].rearrange("p j s -> p s j"),
-                    in1=bT[:, 4 * g:4 * g + 4, s0:s0 + P].rearrange("p j s -> p s j"),
+                    in1=bT[:, g, 2 * half + jl],
                     op=ALU.add,
                 )
                 if jl == 0:
@@ -291,6 +305,7 @@ def tile_mixerblock_pa_kernel(tc, x_proj, mix_mat, mix_b, out_w, out_b, out):
                 out_mm(half, b, obp)
                 out_exit(half, b, obp, both)
 
+        prep_bias()
         x_prep(0)
         load_x(3)
         w_chunk(0, 1)

@@ -53,9 +53,7 @@ def tile_mixerblock_pa_kernel(tc, x_proj, mix_mat, mix_b, out_w, out_b, out):
         osc = keep.tile([P, 2, E], U8, name="osc", align_bytes=64)
         mc = keep.tile([P, 2, B, 2 * HALF], U32, name="mc", align_bytes=64)
         ms = keep.tile([P, 2, B, 2 * HALF], U8, name="ms", align_bytes=64)
-        bT = keep.tile([P, 2, 4, P, 4], BF16, name="bT")
-        mb = keep.tile([P, S], BF16, name="mb")
-        sel = keep.tile([P, 8, P], BF16, name="sel")
+        bT = keep.tile([P, 8, S], BF16, name="bT")
         ident = keep.tile([P, P], BF16, name="ident")
         ones = keep.tile([P, P], F32, name="ones")
         mask = keep.tile([P, P], BF16, name="mask")
@@ -78,33 +76,40 @@ def tile_mixerblock_pa_kernel(tc, x_proj, mix_mat, mix_b, out_w, out_b, out):
                     in_=mix_mat[HC * k:HC * (k + 1), P * j:P * (j + 1), P * j:S].rearrange("h p s -> p h s"),
                 )
 
-        nc.gpsimd.memset(mb[:], 0.0)
-        make_identity(nc, ident[:])
         nc.gpsimd.memset(ones[:], 1.0)
         nc.gpsimd.affine_select(
             out=ones[:], in_=ones[:], pattern=[[1, P]], compare_op=ALU.is_ge,
             fill=0.0, base=0, channel_multiplier=-1,
         )
-        for k in range(NCK):
-            nc.gpsimd.memset(wraw[k][:, :, 3, 2 * P:3 * P], 0.0)
-        nc.gpsimd.memset(obt[:], 0.0)
-        for k in range(NCK):
-            nc.gpsimd.memset(wraw[k][:, :, 1, 0:P], 0.0)
-        for k in range(3):
-            nc.gpsimd.memset(g0[k][:], 0.0)
-        for b in range(B):
+        make_identity(nc, ident[:])
+
+        def zero_x(b):
             nc.vector.memset(
                 xc[b][:].bitcast(I32).rearrange("p (i w) -> p i w", w=PAIRW)[:, :, 64:128], 0)
             nc.vector.memset(
                 xs[b][:].bitcast(I32).rearrange("p (i w) -> p i w", w=PAIRW // 4)[:, :, 16:32], 0)
-        nc.vector.tensor_copy(out=mask[:], in_=ones[:])
 
-        nc.scalar.dma_start(out=mb[0:H, :], in_=mix_b)
+        zero_x(0)
+        for k in range(NCK):
+            nc.vector.memset(wraw[k][:, :, 3, 2 * P:3 * P].bitcast(I32), 0)
+        nc.vector.tensor_copy(out=mask[:], in_=ones[:])
+        for b in range(1, B):
+            zero_x(b)
+        for k in range(NCK):
+            nc.vector.memset(wraw[k][:, :, 1, 0:P].bitcast(I32), 0)
+        for k in range(3):
+            nc.vector.memset(g0[k][:].bitcast(I32), 0)
+        nc.vector.memset(obt[:].bitcast(I32), 0)
+
         load_x(0)
         load_w(0)
         load_w(1)
         load_x(1)
         load_x(2)
+        nc.sync.dma_start(
+            out=bT[0:64, :, :], in_=mix_b.rearrange("(i two) s -> two i s", two=2)[0].partition_broadcast(64))
+        nc.scalar.dma_start(
+            out=bT[64:128, :, :], in_=mix_b.rearrange("(i two) s -> two i s", two=2)[1].partition_broadcast(64))
         load_w(2)
         load_w(3)
         nc.sync.dma_start(out=obt[0:8, :], in_=out_b.rearrange("(r c) -> r c", c=P))
@@ -190,20 +195,6 @@ def tile_mixerblock_pa_kernel(tc, x_proj, mix_mat, mix_b, out_w, out_b, out):
                 in_=og_of[(obp, g)][:].rearrange("p u o j -> p (u o j)"),
             )
 
-        def prep_bias():
-            pairs = ident[:, 0:H].rearrange("p (i two) -> p i two", two=2)
-            for h2 in range(2):
-                nc.vector.tensor_copy(out=sel[:, :, 64 * h2:64 * (h2 + 1)],
-                                      in_=pairs[:, :, h2:h2 + 1].to_broadcast([P, 8, 64]))
-            for g in range(2):
-                for sb in range(4):
-                    pbias = ps1p.tile([P, 4, P], F32, name="acc1")
-                    for j in range(4):
-                        nc.tensor.matmul(out=pbias[:, j, :], lhsT=sel[:, 4 * g + j, :], rhs=mb[:, P * sb:P * (sb + 1)],
-                                         start=True, stop=True)
-                    eng = nc.scalar.copy
-                    eng(out=bT[:, g, sb], in_=pbias[:].rearrange("p j s -> p s j"))
-
         def prep_outb():
             pb = ps2p.tile([P, P], BF16, name="pb", tag="ps2")
             nc.tensor.transpose(pb[:], obt[:], ident[:])
@@ -238,7 +229,7 @@ def tile_mixerblock_pa_kernel(tc, x_proj, mix_mat, mix_b, out_w, out_b, out):
                 nc.vector.tensor_tensor(
                     out=mg[:, P * jl:P * (jl + 1), :],
                     in0=acc1_of[(half, b, g, jl)][:].rearrange("p j s -> p s j"),
-                    in1=bT[:, g, 2 * half + jl],
+                    in1=bT[:, 4 * g:4 * g + 4, s0:s0 + P].rearrange("p j s -> p s j"),
                     op=ALU.add,
                 )
                 if jl == 0:
@@ -305,7 +296,6 @@ def tile_mixerblock_pa_kernel(tc, x_proj, mix_mat, mix_b, out_w, out_b, out):
                 out_mm(half, b, obp)
                 out_exit(half, b, obp, both)
 
-        prep_bias()
         x_prep(0)
         load_x(3)
         w_chunk(0, 1)

@@ -19,7 +19,7 @@ HC = 4
 NCK = H // HC
 PAIRW = 192
 HALF = 256
-ORDER = (1, 0)
+OB = E // P
 
 
 def regroup(eng_copy, dst, src):
@@ -33,9 +33,9 @@ def tile_mixerblock_pa_kernel(tc, x_proj, mix_mat, mix_b, out_w, out_b, out):
     nc = tc.nc
     with ExitStack() as ctx:
         keep = ctx.enter_context(tc.tile_pool(name="keep", bufs=1))
-        rot = ctx.enter_context(tc.tile_pool(name="rot", bufs=3))
+        rot = ctx.enter_context(tc.tile_pool(name="rot", bufs=5))
         xgp = ctx.enter_context(tc.tile_pool(name="xgp", bufs=2))
-        g1p = ctx.enter_context(tc.tile_pool(name="g1p", bufs=3))
+        g1p = ctx.enter_context(tc.tile_pool(name="g1p", bufs=2))
         ogp = ctx.enter_context(tc.tile_pool(name="ogp", bufs=2))
         mgp = ctx.enter_context(tc.tile_pool(name="mgp", bufs=3))
         ps1p = ctx.enter_context(tc.psum_pool(name="ps1p", bufs=4))
@@ -45,20 +45,21 @@ def tile_mixerblock_pa_kernel(tc, x_proj, mix_mat, mix_b, out_w, out_b, out):
         owraw = {}
         xc = [keep.tile([P, 8 * PAIRW], U32, name="xc%d" % b, align_bytes=64) for b in range(B)]
         xs = [keep.tile([P, 8 * PAIRW], U8, name="xs%d" % b, align_bytes=64) for b in range(B)]
-        wraw = [keep.tile([P, HC, 4, S], BF16, name="wraw%d" % k) for k in range(NCK)]
-        g0 = [keep.tile([P, HALF, 4], BF16, name="g0_%d" % k, align_bytes=64) for k in range(3)]
+        w0raw = [keep.tile([P, 2, HC, HALF], BF16, name="w0raw%d" % k) for k in range(NCK)]
+        w1raw = [keep.tile([P, 4, HC, HALF], BF16, name="w1raw%d" % k) for k in range(NCK)]
+        g0 = [keep.tile([P, 2 * HALF, 4], BF16, name="g0_%d" % k, align_bytes=64) for k in range(2)]
         wc = keep.tile([P, 2, H * HALF], U32, name="wc", align_bytes=64)
         ws = keep.tile([P, 2, H * HALF], U8, name="ws", align_bytes=64)
         oc = keep.tile([P, 2, E], U32, name="oc", align_bytes=64)
         osc = keep.tile([P, 2, E], U8, name="osc", align_bytes=64)
         mc = keep.tile([P, 2, B, 2 * HALF], U32, name="mc", align_bytes=64)
         ms = keep.tile([P, 2, B, 2 * HALF], U8, name="ms", align_bytes=64)
-        bT = keep.tile([P, 8, S], BF16, name="bT")
+        bT = [keep.tile([P, 8, HALF], BF16, name="bT%d" % k) for k in range(2)]
         ident = keep.tile([P, P], BF16, name="ident")
         ones = keep.tile([P, P], F32, name="ones")
         mask = keep.tile([P, P], BF16, name="mask")
-        obt = keep.tile([P, P], BF16, name="obt")
-        outb = keep.tile([P, 8], F32, name="outb")
+        outb16 = keep.tile([P, OB], BF16, name="outb16")
+        outb = keep.tile([P, OB], F32, name="outb")
 
         def load_x(b):
             xraw[b] = rot.tile([P, 4, E], BF16, name="xraw", tag="rot")
@@ -67,14 +68,23 @@ def tile_mixerblock_pa_kernel(tc, x_proj, mix_mat, mix_b, out_w, out_b, out):
         def load_ow(q):
             owraw[q] = rot.tile([P, 4, E], BF16, name="owraw", tag="rot")
             nc.sync.dma_start(
-                out=owraw[q][:], in_=out_w[512 * q:512 * (q + 1), :].rearrange("(ob p) c -> p ob c", p=P))
+                out=owraw[q][:], in_=out_w.rearrange("(p ob) c -> p ob c", ob=OB)[:, 4 * q:4 * q + 4, :])
 
-        def load_w(k):
-            for j in range(4):
+        def load_w(k, half):
+            raw = (w0raw, w1raw)[half][k]
+            last = 1 if half == 0 else 3
+            for j in range(last + 1):
+                lo = P if j == last else 0
                 nc.sync.dma_start(
-                    out=wraw[k][:, :, j, P * j:S],
-                    in_=mix_mat[HC * k:HC * (k + 1), P * j:P * (j + 1), P * j:S].rearrange("h p s -> p h s"),
+                    out=raw[:, j, :, lo:HALF],
+                    in_=mix_mat[HC * k:HC * (k + 1), P * j:P * (j + 1),
+                                HALF * half + lo:HALF * (half + 1)].rearrange("h p s -> p h s"),
                 )
+
+        def load_b(half):
+            by_parity = mix_b[:, HALF * half:HALF * (half + 1)].rearrange("(i two) s -> two i s", two=2)
+            nc.sync.dma_start(out=bT[half][0:64, :, :], in_=by_parity[0].partition_broadcast(64))
+            nc.scalar.dma_start(out=bT[half][64:128, :, :], in_=by_parity[1].partition_broadcast(64))
 
         nc.gpsimd.memset(ones[:], 1.0)
         nc.gpsimd.affine_select(
@@ -89,30 +99,30 @@ def tile_mixerblock_pa_kernel(tc, x_proj, mix_mat, mix_b, out_w, out_b, out):
             nc.vector.memset(
                 xs[b][:].bitcast(I32).rearrange("p (i w) -> p i w", w=PAIRW // 4)[:, :, 16:32], 0)
 
-        zero_x(0)
-        for k in range(NCK):
-            nc.vector.memset(wraw[k][:, :, 3, 2 * P:3 * P].bitcast(I32), 0)
-        nc.vector.tensor_copy(out=mask[:], in_=ones[:])
-        for b in range(1, B):
-            zero_x(b)
-        for k in range(NCK):
-            nc.vector.memset(wraw[k][:, :, 1, 0:P].bitcast(I32), 0)
-        for k in range(3):
-            nc.vector.memset(g0[k][:].bitcast(I32), 0)
-        nc.vector.memset(obt[:].bitcast(I32), 0)
+        def zero_w(half):
+            for k in range(NCK):
+                raw = (w0raw, w1raw)[half][k]
+                nc.vector.memset(raw[:, 2 * half + 1, :, 0:P].bitcast(I32), 0)
 
+        zero_w(0)
+        nc.vector.tensor_copy(out=mask[:], in_=ones[:])
+        for k in range(2):
+            nc.vector.memset(g0[k][:].bitcast(I32), 0)
+        zero_x(0)
+
+        load_w(0, 0)
         load_x(0)
-        load_w(0)
-        load_w(1)
+        load_w(1, 0)
+        load_w(2, 0)
+        load_w(3, 0)
+        load_ow(0)
+        load_ow(1)
+        load_b(0)
         load_x(1)
         load_x(2)
-        nc.sync.dma_start(
-            out=bT[0:64, :, :], in_=mix_b.rearrange("(i two) s -> two i s", two=2)[0].partition_broadcast(64))
-        nc.scalar.dma_start(
-            out=bT[64:128, :, :], in_=mix_b.rearrange("(i two) s -> two i s", two=2)[1].partition_broadcast(64))
-        load_w(2)
-        load_w(3)
-        nc.sync.dma_start(out=obt[0:8, :], in_=out_b.rearrange("(r c) -> r c", c=P))
+        load_w(0, 1)
+        load_w(1, 1)
+        nc.sync.dma_start(out=outb16[:], in_=out_b.rearrange("(p ob) -> p ob", ob=OB))
 
         xg_of = {}
 
@@ -121,8 +131,7 @@ def tile_mixerblock_pa_kernel(tc, x_proj, mix_mat, mix_b, out_w, out_b, out):
             xg_of[(b, ch)] = xg
             c_lo = 512 * ch
             for q in range(2):
-                eng = nc.vector.tensor_copy if (b == 0 and q == 0) else nc.scalar.copy
-                regroup(eng, xg[:, 256 * q:256 * (q + 1), :],
+                regroup(nc.scalar.copy, xg[:, 256 * q:256 * (q + 1), :],
                         xraw[b][:, :, c_lo + 256 * q:c_lo + 256 * (q + 1)])
 
         def x_quant(b, ch):
@@ -138,13 +147,11 @@ def tile_mixerblock_pa_kernel(tc, x_proj, mix_mat, mix_b, out_w, out_b, out):
                     in_=flat[:, 4 * c0:4 * c1],
                 )
 
-        def w_mask(k, slots):
-            for j in slots:
-                d = wraw[k][:, :, j, P * j:P * (j + 1)]
+        def w_mask(k, half):
+            for j in range(2):
+                d = (w0raw, w1raw)[half][k][:, 2 * half + j, :, P * j:P * (j + 1)]
                 nc.vector.tensor_tensor(
                     out=d, in0=d, in1=mask[:].unsqueeze(1).to_broadcast([P, HC, P]), op=ALU.mult)
-
-        g_of = {}
 
         late_w = []
         late_m = []
@@ -158,17 +165,20 @@ def tile_mixerblock_pa_kernel(tc, x_proj, mix_mat, mix_b, out_w, out_b, out):
             flush(late)
             late.append(call)
 
-        def w_prep(h, half):
+        def w_prep(hp, half):
+            k, r = divmod(2 * hp, HC)
             if half == 1:
-                g = g1p.tile([P, HALF, 4], BF16, name="g1", align_bytes=64)
-                eng = nc.vector.tensor_copy if h % 4 == 0 else nc.scalar.copy
-                regroup(eng, g[:], wraw[h // HC][:, h % HC, :, HALF:2 * HALF])
+                g = g1p.tile([P, 2 * HALF, 4], BF16, name="g1", align_bytes=64)
+                eng = nc.vector.tensor_copy if hp % 2 == 0 else nc.scalar.copy
+                regroup(eng, g[:], w1raw[k][:, :, r:r + 2, :].rearrange("p t h s -> p t (h s)"))
             else:
-                g = g0[h % 3]
-                regroup(nc.vector.tensor_copy, g[:, :, 0:2], wraw[h // HC][:, h % HC, 0:2, 0:HALF])
+                g = g0[hp % 2]
+                eng = nc.scalar.copy if hp % 4 == 3 else nc.vector.tensor_copy
+                regroup(eng, g[:, :, 0:2], w0raw[k][:, :, r:r + 2, :].rearrange("p t h s -> p t (h s)"))
+            w0 = 2 * hp * HALF
             defer(late_w, lambda: nc.vector.quantize_mx(
-                out=wc[:, half, h * HALF:(h + 1) * HALF].bitcast(FP8X4),
-                scales=ws[:, half, h * HALF:(h + 1) * HALF],
+                out=wc[:, half, w0:w0 + 2 * HALF].bitcast(FP8X4),
+                scales=ws[:, half, w0:w0 + 2 * HALF],
                 in_=g[:].rearrange("p s t -> p (s t)"),
             ))
 
@@ -195,11 +205,6 @@ def tile_mixerblock_pa_kernel(tc, x_proj, mix_mat, mix_b, out_w, out_b, out):
                 in_=og_of[(obp, g)][:].rearrange("p u o j -> p (u o j)"),
             )
 
-        def prep_outb():
-            pb = ps2p.tile([P, P], BF16, name="pb", tag="ps2")
-            nc.tensor.transpose(pb[:], obt[:], ident[:])
-            nc.vector.tensor_copy(out=outb[:], in_=pb[:, 0:8])
-
         acc1_of = {}
 
         def mix_mm(half, b, g):
@@ -225,11 +230,10 @@ def tile_mixerblock_pa_kernel(tc, x_proj, mix_mat, mix_b, out_w, out_b, out):
         def mix_exit(half, b, g):
             mg = mgp.tile([P, HALF, 4], BF16, name="mg", align_bytes=64)
             for jl in range(2):
-                s0 = HALF * half + P * jl
                 nc.vector.tensor_tensor(
                     out=mg[:, P * jl:P * (jl + 1), :],
                     in0=acc1_of[(half, b, g, jl)][:].rearrange("p j s -> p s j"),
-                    in1=bT[:, 4 * g:4 * g + 4, s0:s0 + P].rearrange("p j s -> p s j"),
+                    in1=bT[half][:, 4 * g:4 * g + 4, P * jl:P * (jl + 1)].rearrange("p j s -> p s j"),
                     op=ALU.add,
                 )
                 if jl == 0:
@@ -263,7 +267,7 @@ def tile_mixerblock_pa_kernel(tc, x_proj, mix_mat, mix_b, out_w, out_b, out):
 
         def out_exit(half, b, obp, both):
             if obp == 0:
-                ot_of[0] = rot.tile([P, 8, HALF], F32, name="ot8", tag="rot")
+                ot_of[0] = rot.tile([P, OB, HALF], F32, name="ot8", tag="rot")
             acc = acc2_of[(half, b, obp)]
             for u in range(2):
                 ob = 2 * obp + u
@@ -273,7 +277,7 @@ def tile_mixerblock_pa_kernel(tc, x_proj, mix_mat, mix_b, out_w, out_b, out):
                 else:
                     nc.scalar.activation(out=ot, in_=acc[:, u, :], func=ACT.Identity, bias=outb[:, ob:ob + 1], scale=1.0)
             nc.sync.dma_start(
-                out=out[b, 2 * P * obp:2 * P * (obp + 1), HALF * half:HALF * (half + 1)].rearrange("(u p) s -> p u s", p=P),
+                out=out[b].rearrange("(p ob) s -> p ob s", ob=OB)[:, 2 * obp:2 * obp + 2, HALF * half:HALF * (half + 1)],
                 in_=ot_of[0][:, 2 * obp:2 * obp + 2, :],
             )
 
@@ -283,9 +287,9 @@ def tile_mixerblock_pa_kernel(tc, x_proj, mix_mat, mix_b, out_w, out_b, out):
                 x_quant(b, ch)
 
         def w_chunk(k, half):
-            w_mask(k, (2, 3) if half == 1 else (0, 1))
-            for h in range(HC * k, HC * (k + 1)):
-                w_prep(h, half)
+            w_mask(k, half)
+            for hp in range(2 * k, 2 * k + 2):
+                w_prep(hp, half)
 
         def mix(half, b, g):
             mix_mm(half, b, g)
@@ -296,41 +300,46 @@ def tile_mixerblock_pa_kernel(tc, x_proj, mix_mat, mix_b, out_w, out_b, out):
                 out_mm(half, b, obp)
                 out_exit(half, b, obp, both)
 
-        x_prep(0)
-        load_x(3)
-        w_chunk(0, 1)
-        w_chunk(1, 1)
-        mix(1, 0, 0)
         w_chunk(0, 0)
+        x_prep(0)
         w_chunk(1, 0)
-        x_prep(1)
-        load_ow(0)
-        mix(1, 1, 0)
-        x_prep(2)
-        load_ow(1)
-        mix(1, 2, 0)
-        w_chunk(2, 1)
-        w_chunk(3, 1)
-        mix(1, 0, 1)
-        mix(1, 1, 1)
-        prep_outb()
+        mix(0, 0, 0)
+        w_chunk(2, 0)
+        w_chunk(3, 0)
+        mix(0, 0, 1)
         for obp in range(4):
             for g in range(2):
                 ow_transpose(obp, g)
                 ow_exit(obp, g)
                 ow_quant(obp, g)
-        project(1, 0, False)
-        project(1, 1, False)
+        nc.vector.tensor_copy(out=outb[:], in_=outb16[:])
+        load_x(3)
+        load_w(2, 1)
+        load_w(3, 1)
+        load_b(1)
+        project(0, 0, False)
+        zero_x(1)
+        x_prep(1)
+        mix(0, 1, 0)
+        mix(0, 1, 1)
+        project(0, 1, False)
+        zero_x(2)
+        x_prep(2)
+        mix(0, 2, 0)
+        mix(0, 2, 1)
+        project(0, 2, False)
+        zero_w(1)
+        w_chunk(0, 1)
+        w_chunk(1, 1)
+        zero_x(3)
         x_prep(3)
-        mix(1, 2, 1)
-        project(1, 2, False)
-        mix(1, 3, 0)
-        mix(1, 3, 1)
-        project(1, 3, False)
+        mix(0, 3, 0)
+        mix(0, 3, 1)
+        project(0, 3, False)
         for b in range(B):
-            mix(0, b, 0)
-        w_chunk(2, 0)
-        w_chunk(3, 0)
+            mix(1, b, 0)
+        w_chunk(2, 1)
+        w_chunk(3, 1)
         for b in range(B):
-            mix(0, b, 1)
-            project(0, b, b == 3)
+            mix(1, b, 1)
+            project(1, b, b == 3)

@@ -54,9 +54,10 @@ def tile_mixerblock_pa_kernel(tc, x_proj, mix_mat, mix_b, out_w, out_b, out):
         osc = keep.tile([P, 2, E], U8, name="osc", align_bytes=64)
         mc = keep.tile([P, 2, B, 2 * HALF], U32, name="mc", align_bytes=64)
         ms = keep.tile([P, 2, B, 2 * HALF], U8, name="ms", align_bytes=64)
-        bT = [keep.tile([P, 8, HALF], BF16, name="bT%d" % k) for k in range(2)]
+        bT = keep.tile([P, 2, 2, HALF, 4], BF16, name="bT")
+        mb = keep.tile([P, S], BF16, name="mb")
+        sel = keep.tile([P, H, E // H], BF16, name="sel")
         ident = keep.tile([P, P], BF16, name="ident")
-        ones = keep.tile([P, P], F32, name="ones")
         mask = keep.tile([P, P], BF16, name="mask")
         outb16 = keep.tile([P, OB], BF16, name="outb16")
         outb = keep.tile([P, OB], F32, name="outb")
@@ -81,58 +82,66 @@ def tile_mixerblock_pa_kernel(tc, x_proj, mix_mat, mix_b, out_w, out_b, out):
                                 HALF * half + lo:HALF * (half + 1)].rearrange("h p s -> p h s"),
                 )
 
-        def load_b(half):
-            by_parity = mix_b[:, HALF * half:HALF * (half + 1)].rearrange("(i two) s -> two i s", two=2)
-            nc.sync.dma_start(out=bT[half][0:64, :, :], in_=by_parity[0].partition_broadcast(64))
-            nc.scalar.dma_start(out=bT[half][64:128, :, :], in_=by_parity[1].partition_broadcast(64))
+        def spread_b(half, g):
+            pb = ps2p.tile([P, 4, HALF], BF16, name="pb", tag="ps2")
+            for j in range(4):
+                i = 4 * g + j
+                nc.tensor.matmul(
+                    pb[:, j, :], lhsT=sel[:, 2 * i:2 * i + 2, :].rearrange("p h e -> p (h e)"),
+                    rhs=mb[:, HALF * half:HALF * (half + 1)], start=True, stop=True)
+            nc.scalar.copy(out=bT[:, half, g, :, :], in_=pb[:].rearrange("p j s -> p s j"))
 
-        nc.gpsimd.memset(ones[:], 1.0)
+        ctx.enter_context(tc.manual_schedule())
+        make_identity(nc, ident[:])
+        nc.gpsimd.memset(mask[:], 1.0)
         nc.gpsimd.affine_select(
-            out=ones[:], in_=ones[:], pattern=[[1, P]], compare_op=ALU.is_ge,
+            out=mask[:], in_=mask[:], pattern=[[1, P]], compare_op=ALU.is_ge,
             fill=0.0, base=0, channel_multiplier=-1,
         )
-        make_identity(nc, ident[:])
 
-        def zero_x(b):
-            nc.vector.memset(
+        def zero_x(eng, b):
+            eng.memset(
                 xc[b][:].bitcast(I32).rearrange("p (i w) -> p i w", w=PAIRW)[:, :, 64:128], 0)
-            nc.vector.memset(
+            eng.memset(
                 xs[b][:].bitcast(I32).rearrange("p (i w) -> p i w", w=PAIRW // 4)[:, :, 16:32], 0)
 
-        def zero_w(half):
+        def zero_w(eng, half):
             for k in range(NCK):
                 raw = (w0raw, w1raw)[half][k]
-                nc.vector.memset(raw[:, 2 * half + 1, :, 0:P].bitcast(I32), 0)
+                eng.memset(raw[:, 2 * half + 1, :, 0:P].bitcast(I32), 0)
 
-        zero_w(0)
-        nc.vector.tensor_copy(out=mask[:], in_=ones[:])
+        nc.vector.memset(mb[:].bitcast(I32), 0)
+        zero_w(nc.vector, 0)
+        zero_x(nc.gpsimd, 1)
+        zero_w(nc.gpsimd, 1)
+        zero_x(nc.gpsimd, 2)
+        zero_x(nc.gpsimd, 3)
+        nc.vector.tensor_copy(out=sel[:], in_=ident[:, 0:H].unsqueeze(2).to_broadcast([P, H, E // H]))
         for k in range(2):
-            nc.vector.memset(g0[k][:].bitcast(I32), 0)
-        zero_x(0)
+            nc.vector.memset(g0[k][:].rearrange("p s t -> p (s t)").bitcast(I32).rearrange("p (s w) -> p s w", w=2)[:, :, 1:2], 0)
+        zero_x(nc.vector, 0)
 
+        nc.sync.dma_start(out=mb[0:H, :], in_=mix_b)
         load_w(0, 0)
         load_x(0)
         load_w(1, 0)
         load_w(2, 0)
         load_w(3, 0)
+        load_x(1)
         load_ow(0)
         load_ow(1)
-        load_b(0)
-        load_x(1)
         load_x(2)
-        load_w(0, 1)
-        load_w(1, 1)
         nc.sync.dma_start(out=outb16[:], in_=out_b.rearrange("(p ob) -> p ob", ob=OB))
+        for k in range(NCK):
+            load_w(k, 1)
+        load_x(3)
 
         xg_of = {}
 
         def x_regroup(b, ch):
             xg = xgp.tile([P, 512, 4], BF16, name="xg", align_bytes=64)
             xg_of[(b, ch)] = xg
-            c_lo = 512 * ch
-            for q in range(2):
-                regroup(nc.scalar.copy, xg[:, 256 * q:256 * (q + 1), :],
-                        xraw[b][:, :, c_lo + 256 * q:c_lo + 256 * (q + 1)])
+            regroup(nc.scalar.copy, xg[:], xraw[b][:, :, 512 * ch:512 * (ch + 1)])
 
         def x_quant(b, ch):
             flat = xg_of[(b, ch)][:].rearrange("p c t -> p (c t)")
@@ -153,34 +162,25 @@ def tile_mixerblock_pa_kernel(tc, x_proj, mix_mat, mix_b, out_w, out_b, out):
                 nc.vector.tensor_tensor(
                     out=d, in0=d, in1=mask[:].unsqueeze(1).to_broadcast([P, HC, P]), op=ALU.mult)
 
-        late_w = []
-        late_m = []
+        g_of = {}
 
-        def flush(late):
-            for call in late:
-                call()
-            late[0:len(late)] = []
-
-        def defer(late, call):
-            flush(late)
-            late.append(call)
-
-        def w_prep(hp, half):
+        def w_regroup(eng_copy, hp, half):
             k, r = divmod(2 * hp, HC)
             if half == 1:
                 g = g1p.tile([P, 2 * HALF, 4], BF16, name="g1", align_bytes=64)
-                eng = nc.vector.tensor_copy if hp % 2 == 0 else nc.scalar.copy
-                regroup(eng, g[:], w1raw[k][:, :, r:r + 2, :].rearrange("p t h s -> p t (h s)"))
+                regroup(eng_copy, g[:], w1raw[k][:, :, r:r + 2, :].rearrange("p t h s -> p t (h s)"))
             else:
                 g = g0[hp % 2]
-                eng = nc.scalar.copy if hp % 4 == 3 else nc.vector.tensor_copy
-                regroup(eng, g[:, :, 0:2], w0raw[k][:, :, r:r + 2, :].rearrange("p t h s -> p t (h s)"))
+                regroup(eng_copy, g[:, :, 0:2], w0raw[k][:, :, r:r + 2, :].rearrange("p t h s -> p t (h s)"))
+            g_of[(hp, half)] = g
+
+        def w_quant(hp, half):
             w0 = 2 * hp * HALF
-            defer(late_w, lambda: nc.vector.quantize_mx(
+            nc.vector.quantize_mx(
                 out=wc[:, half, w0:w0 + 2 * HALF].bitcast(FP8X4),
                 scales=ws[:, half, w0:w0 + 2 * HALF],
-                in_=g[:].rearrange("p s t -> p (s t)"),
-            ))
+                in_=g_of[(hp, half)][:].rearrange("p s t -> p (s t)"),
+            )
 
         pt_of = {}
         og_of = {}
@@ -208,7 +208,6 @@ def tile_mixerblock_pa_kernel(tc, x_proj, mix_mat, mix_b, out_w, out_b, out):
         acc1_of = {}
 
         def mix_mm(half, b, g):
-            flush(late_w)
             for jl in range(2):
                 acc = ps1p.tile([P, 4, P], F32, name="acc1")
                 acc1_of[(half, b, g, jl)] = acc
@@ -227,27 +226,29 @@ def tile_mixerblock_pa_kernel(tc, x_proj, mix_mat, mix_b, out_w, out_b, out):
                             stop=(h2 == 1),
                         )
 
+        mg_of = {}
+
         def mix_exit(half, b, g):
             mg = mgp.tile([P, HALF, 4], BF16, name="mg", align_bytes=64)
+            mg_of[(half, b, g)] = mg
             for jl in range(2):
                 nc.vector.tensor_tensor(
                     out=mg[:, P * jl:P * (jl + 1), :],
                     in0=acc1_of[(half, b, g, jl)][:].rearrange("p j s -> p s j"),
-                    in1=bT[half][:, 4 * g:4 * g + 4, P * jl:P * (jl + 1)].rearrange("p j s -> p s j"),
+                    in1=bT[:, half, g, P * jl:P * (jl + 1), :],
                     op=ALU.add,
                 )
-                if jl == 0:
-                    flush(late_m)
-            late_m.append(lambda: nc.vector.quantize_mx(
+
+        def mix_quant(half, b, g):
+            nc.vector.quantize_mx(
                 out=mc[:, half, b, HALF * g:HALF * (g + 1)].bitcast(FP8X4),
                 scales=ms[:, half, b, HALF * g:HALF * (g + 1)],
-                in_=mg[:].rearrange("p s j -> p (s j)"),
-            ))
+                in_=mg_of[(half, b, g)][:].rearrange("p s j -> p (s j)"),
+            )
 
         acc2_of = {}
 
         def out_mm(half, b, obp):
-            flush(late_m)
             acc = ps2p.tile([P, 2, HALF], F32, name="acc2", tag="ps2")
             acc2_of[(half, b, obp)] = acc
             for u in range(2):
@@ -281,65 +282,148 @@ def tile_mixerblock_pa_kernel(tc, x_proj, mix_mat, mix_b, out_w, out_b, out):
                 in_=ot_of[0][:, 2 * obp:2 * obp + 2, :],
             )
 
-        def x_prep(b):
-            for ch in range(2):
-                x_regroup(b, ch)
-                x_quant(b, ch)
+        v, s = nc.vector.tensor_copy, nc.scalar.copy
 
-        def w_chunk(k, half):
-            w_mask(k, half)
-            for hp in range(2 * k, 2 * k + 2):
-                w_prep(hp, half)
-
-        def mix(half, b, g):
-            mix_mm(half, b, g)
-            mix_exit(half, b, g)
-
-        def project(half, b, both):
+        def project(half, b, both=False):
             for obp in range(4):
                 out_mm(half, b, obp)
                 out_exit(half, b, obp, both)
 
-        w_chunk(0, 0)
-        x_prep(0)
-        w_chunk(1, 0)
-        mix(0, 0, 0)
-        w_chunk(2, 0)
-        w_chunk(3, 0)
-        mix(0, 0, 1)
-        for obp in range(4):
+        for half in range(2):
+            for g in range(2):
+                spread_b(half, g)
+        w_mask(0, 0)
+        w_regroup(v, 0, 0)
+        w_regroup(s, 1, 0)
+        x_regroup(0, 0)
+        w_quant(0, 0)
+        w_mask(1, 0)
+        w_regroup(v, 2, 0)
+        w_quant(1, 0)
+        w_regroup(s, 3, 0)
+        x_regroup(0, 1)
+        w_quant(2, 0)
+        x_quant(0, 0)
+        w_mask(2, 0)
+        w_quant(3, 0)
+        mix_mm(0, 0, 0)
+        w_regroup(v, 4, 0)
+        w_regroup(s, 5, 0)
+        w_mask(3, 0)
+        w_quant(4, 0)
+        mix_exit(0, 0, 0)
+        x_quant(0, 1)
+        w_quant(5, 0)
+        w_regroup(v, 6, 0)
+        w_regroup(s, 7, 0)
+        mix_quant(0, 0, 0)
+        w_quant(6, 0)
+        w_quant(7, 0)
+        mix_mm(0, 0, 1)
+        x_regroup(1, 0)
+        x_regroup(1, 1)
+        for obp in range(2):
             for g in range(2):
                 ow_transpose(obp, g)
-                ow_exit(obp, g)
-                ow_quant(obp, g)
+        mix_exit(0, 0, 1)
+        x_quant(1, 0)
+        mix_mm(0, 1, 0)
+        mix_quant(0, 0, 1)
+        ow_exit(0, 0)
+        ow_exit(0, 1)
+        x_quant(1, 1)
+        ow_exit(1, 0)
+        ow_exit(1, 1)
+        for obp in range(2, 4):
+            for g in range(2):
+                ow_transpose(obp, g)
+        mix_exit(0, 1, 0)
+        ow_quant(0, 0)
+        ow_quant(0, 1)
+        mix_mm(0, 1, 1)
+        ow_exit(2, 0)
+        ow_exit(2, 1)
+        mix_quant(0, 1, 0)
+        ow_quant(1, 0)
+        ow_quant(1, 1)
+        ow_exit(3, 0)
+        ow_exit(3, 1)
+        mix_exit(0, 1, 1)
+        ow_quant(2, 0)
+        ow_quant(2, 1)
+        mix_quant(0, 1, 1)
         nc.vector.tensor_copy(out=outb[:], in_=outb16[:])
-        load_x(3)
-        load_w(2, 1)
-        load_w(3, 1)
-        load_b(1)
-        project(0, 0, False)
-        zero_x(1)
-        x_prep(1)
-        mix(0, 1, 0)
-        mix(0, 1, 1)
-        project(0, 1, False)
-        zero_x(2)
-        x_prep(2)
-        mix(0, 2, 0)
-        mix(0, 2, 1)
-        project(0, 2, False)
-        zero_w(1)
-        w_chunk(0, 1)
-        w_chunk(1, 1)
-        zero_x(3)
-        x_prep(3)
-        mix(0, 3, 0)
-        mix(0, 3, 1)
-        project(0, 3, False)
-        for b in range(B):
-            mix(1, b, 0)
-        w_chunk(2, 1)
-        w_chunk(3, 1)
-        for b in range(B):
-            mix(1, b, 1)
-            project(1, b, b == 3)
+        w_mask(0, 1)
+        ow_quant(3, 0)
+        ow_quant(3, 1)
+        x_regroup(2, 0)
+        w_regroup(v, 0, 1)
+        project(0, 0)
+        w_regroup(v, 1, 1)
+        w_quant(0, 1)
+        w_mask(1, 1)
+        x_regroup(2, 1)
+        x_quant(2, 0)
+        w_quant(1, 1)
+        mix_mm(0, 2, 0)
+        project(0, 1)
+        w_regroup(v, 2, 1)
+        x_quant(2, 1)
+        mix_exit(0, 2, 0)
+        w_quant(2, 1)
+        mix_mm(0, 2, 1)
+        w_regroup(s, 3, 1)
+        w_mask(2, 1)
+        mix_quant(0, 2, 0)
+        w_regroup(v, 4, 1)
+        mix_exit(0, 2, 1)
+        w_quant(3, 1)
+        mix_mm(1, 0, 0)
+        mix_mm(1, 1, 0)
+        mix_quant(0, 2, 1)
+        w_regroup(s, 5, 1)
+        w_quant(4, 1)
+        w_mask(3, 1)
+        mix_exit(1, 0, 0)
+        project(0, 2)
+        w_regroup(v, 6, 1)
+        mix_quant(1, 0, 0)
+        mix_exit(1, 1, 0)
+        mix_mm(1, 2, 0)
+        w_regroup(s, 7, 1)
+        w_quant(5, 1)
+        mix_quant(1, 1, 0)
+        w_quant(6, 1)
+        mix_exit(1, 2, 0)
+        x_regroup(3, 0)
+        w_quant(7, 1)
+        mix_mm(1, 0, 1)
+        mix_quant(1, 2, 0)
+        mix_mm(1, 1, 1)
+        mix_exit(1, 0, 1)
+        x_quant(3, 0)
+        mix_quant(1, 0, 1)
+        mix_exit(1, 1, 1)
+        x_regroup(3, 1)
+        mix_mm(0, 3, 0)
+        project(1, 0)
+        mix_quant(1, 1, 1)
+        mix_exit(0, 3, 0)
+        x_quant(3, 1)
+        mix_mm(1, 2, 1)
+        project(1, 1)
+        mix_quant(0, 3, 0)
+        mix_exit(1, 2, 1)
+        mix_mm(0, 3, 1)
+        mix_quant(1, 2, 1)
+        mix_exit(0, 3, 1)
+        mix_mm(1, 3, 0)
+        project(1, 2)
+        mix_quant(0, 3, 1)
+        mix_exit(1, 3, 0)
+        mix_mm(1, 3, 1)
+        mix_quant(1, 3, 0)
+        project(0, 3)
+        mix_exit(1, 3, 1)
+        mix_quant(1, 3, 1)
+        project(1, 3, True)

@@ -45,8 +45,14 @@ def tile_mixerblock_pa_kernel(tc, x_proj, mix_mat, mix_b, out_w, out_b, out):
         owraw = {}
         xc = [keep.tile([P, 8 * PAIRW], U32, name="xc%d" % b, align_bytes=64) for b in range(B)]
         xs = [keep.tile([P, 8 * PAIRW], U8, name="xs%d" % b, align_bytes=64) for b in range(B)]
-        w0raw = [keep.tile([P, 2, HC, HALF], BF16, name="w0raw%d" % k) for k in range(NCK)]
-        w1raw = [keep.tile([P, 4, HC, HALF], BF16, name="w1raw%d" % k) for k in range(NCK)]
+        w0raw = [keep.tile([P, 2 * HC * HALF + 2 * P], BF16, name="w0raw%d" % k) for k in range(NCK)]
+        w1buf = [keep.tile([P, 4 * HC * HALF + 2 * P], BF16, name="w1raw%d" % k) for k in range(3)]
+        w1raw = [w1buf[k % 3] for k in range(NCK)]
+
+        def slots(k, half):
+            return (w0raw, w1raw)[half][k][:, 0:(2 + 2 * half) * HC * HALF].rearrange(
+                "p (j h s) -> p j h s", h=HC, s=HALF)
+
         g0 = [keep.tile([P, 2 * HALF, 4], BF16, name="g0_%d" % k, align_bytes=64) for k in range(2)]
         wc = keep.tile([P, 2, H * HALF], U32, name="wc", align_bytes=64)
         ws = keep.tile([P, 2, H * HALF], U8, name="ws", align_bytes=64)
@@ -55,8 +61,8 @@ def tile_mixerblock_pa_kernel(tc, x_proj, mix_mat, mix_b, out_w, out_b, out):
         mc = keep.tile([P, 2, B, 2 * HALF], U32, name="mc", align_bytes=64)
         ms = keep.tile([P, 2, B, 2 * HALF], U8, name="ms", align_bytes=64)
         bT = keep.tile([P, 2, 2, HALF, 4], BF16, name="bT")
-        mb = keep.tile([P, S], BF16, name="mb")
-        sel = keep.tile([P, H, E // H], BF16, name="sel")
+        mb = ogp.tile([P, S], BF16, name="mb", tag="og", align_bytes=64)
+        sel = ogp.tile([P, H, E // H], BF16, name="sel", tag="og", align_bytes=64)
         ident = keep.tile([P, P], BF16, name="ident")
         mask = keep.tile([P, P], BF16, name="mask")
         outb16 = keep.tile([P, OB], BF16, name="outb16")
@@ -72,7 +78,7 @@ def tile_mixerblock_pa_kernel(tc, x_proj, mix_mat, mix_b, out_w, out_b, out):
                 out=owraw[q][:], in_=out_w.rearrange("(p ob) c -> p ob c", ob=OB)[:, 4 * q:4 * q + 4, :])
 
         def load_w(k, half):
-            raw = (w0raw, w1raw)[half][k]
+            raw = slots(k, half)
             last = 1 if half == 0 else 3
             for j in range(last + 1):
                 lo = P if j == last else 0
@@ -106,9 +112,8 @@ def tile_mixerblock_pa_kernel(tc, x_proj, mix_mat, mix_b, out_w, out_b, out):
                 xs[b][:].bitcast(I32).rearrange("p (i w) -> p i w", w=PAIRW // 4)[:, :, 16:32], 0)
 
         def zero_w(eng, half):
-            for k in range(NCK):
-                raw = (w0raw, w1raw)[half][k]
-                eng.memset(raw[:, 2 * half + 1, :, 0:P].bitcast(I32), 0)
+            for k in range(3 if half else NCK):
+                eng.memset(slots(k, half)[:, 2 * half + 1, :, 0:P].bitcast(I32), 0)
 
         nc.vector.memset(mb[:].bitcast(I32), 0)
         zero_w(nc.vector, 0)
@@ -132,35 +137,41 @@ def tile_mixerblock_pa_kernel(tc, x_proj, mix_mat, mix_b, out_w, out_b, out):
         load_ow(1)
         load_x(2)
         nc.sync.dma_start(out=outb16[:], in_=out_b.rearrange("(p ob) -> p ob", ob=OB))
-        for k in range(NCK):
+        for k in range(3):
             load_w(k, 1)
         load_x(3)
 
         xg_of = {}
 
+        XCUT = (0, 576, 1024)
+
         def x_regroup(b, ch):
-            xg = xgp.tile([P, 512, 4], BF16, name="xg", align_bytes=64)
+            lo, hi = XCUT[ch], XCUT[ch + 1]
+            xg = xgp.tile([P, 576, 4], BF16, name="xg", align_bytes=64)
             xg_of[(b, ch)] = xg
-            regroup(nc.scalar.copy, xg[:], xraw[b][:, :, 512 * ch:512 * (ch + 1)])
+            regroup(nc.scalar.copy, xg[:, 0:hi - lo, :], xraw[b][:, :, lo:hi])
 
         def x_quant(b, ch):
+            lo, hi = XCUT[ch], XCUT[ch + 1]
             flat = xg_of[(b, ch)][:].rearrange("p c t -> p (c t)")
-            w_lo = PAIRW * 4 * ch
-            spans = [(0, 64, w_lo)]
-            spans.extend((P * i + 64, P * i + 192, w_lo + PAIRW * i + P) for i in range(3))
-            spans.append((448, 512, w_lo + PAIRW * 3 + P))
-            for c0, c1, w0 in spans:
+            c0 = lo
+            while c0 < hi:
+                c1 = min(c0 + P if c0 % P else c0 + 64, hi)
+                w0 = PAIRW * (c0 // P) + (P if c0 % P else 0)
                 nc.vector.quantize_mx(
                     out=xc[b][:, w0:w0 + c1 - c0].bitcast(FP8X4),
                     scales=xs[b][:, w0:w0 + c1 - c0],
-                    in_=flat[:, 4 * c0:4 * c1],
+                    in_=flat[:, 4 * (c0 - lo):4 * (c1 - lo)],
                 )
+                c0 = c1
 
         def w_mask(k, half):
-            for j in range(2):
-                d = (w0raw, w1raw)[half][k][:, 2 * half + j, :, P * j:P * (j + 1)]
-                nc.vector.tensor_tensor(
-                    out=d, in0=d, in1=mask[:].unsqueeze(1).to_broadcast([P, HC, P]), op=ALU.mult)
+            step = HC * HALF + P
+            lo = 2 * half * HC * HALF
+            d = (w0raw, w1raw)[half][k][:, lo:lo + 2 * step].rearrange("p (j x) -> p j x", x=step)
+            d = d[:, :, 0:HC * HALF].rearrange("p j (h s) -> p j h s", s=HALF)[:, :, :, 0:P]
+            nc.vector.tensor_tensor(
+                out=d, in0=d, in1=mask[:].unsqueeze(1).unsqueeze(1).to_broadcast([P, 2, HC, P]), op=ALU.mult)
 
         g_of = {}
 
@@ -168,10 +179,10 @@ def tile_mixerblock_pa_kernel(tc, x_proj, mix_mat, mix_b, out_w, out_b, out):
             k, r = divmod(2 * hp, HC)
             if half == 1:
                 g = g1p.tile([P, 2 * HALF, 4], BF16, name="g1", align_bytes=64)
-                regroup(eng_copy, g[:], w1raw[k][:, :, r:r + 2, :].rearrange("p t h s -> p t (h s)"))
+                regroup(eng_copy, g[:], slots(k, 1)[:, :, r:r + 2, :].rearrange("p t h s -> p t (h s)"))
             else:
                 g = g0[hp % 2]
-                regroup(eng_copy, g[:, :, 0:2], w0raw[k][:, :, r:r + 2, :].rearrange("p t h s -> p t (h s)"))
+                regroup(eng_copy, g[:, :, 0:2], slots(k, 0)[:, :, r:r + 2, :].rearrange("p t h s -> p t (h s)"))
             g_of[(hp, half)] = g
 
         def w_quant(hp, half):
@@ -194,15 +205,16 @@ def tile_mixerblock_pa_kernel(tc, x_proj, mix_mat, mix_b, out_w, out_b, out):
                     nc.tensor.transpose(pt[:, u, j, :], owraw[obp // 2][:, 2 * (obp % 2) + u, c0:c0 + P], ident[:])
 
         def ow_exit(obp, g):
-            og = ogp.tile([P, 2, P, 4], BF16, name="og", align_bytes=64)
-            og_of[(obp, g)] = og
-            nc.scalar.copy(out=og[:], in_=pt_of[(obp, g)][:].rearrange("p u j o -> p u o j"))
+            if obp % 2 == 0:
+                og_of[(obp // 2, g)] = ogp.tile([P, 4, P, 4], BF16, name="og", align_bytes=64)
+            u0 = 2 * (obp % 2)
+            nc.scalar.copy(out=og_of[(obp // 2, g)][:, u0:u0 + 2, :, :], in_=pt_of[(obp, g)][:].rearrange("p u j o -> p u o j"))
 
-        def ow_quant(obp, g):
+        def ow_quant(q, g):
             nc.vector.quantize_mx(
-                out=oc[:, g, 2 * P * obp:2 * P * (obp + 1)].bitcast(FP8X4),
-                scales=osc[:, g, 2 * P * obp:2 * P * (obp + 1)],
-                in_=og_of[(obp, g)][:].rearrange("p u o j -> p (u o j)"),
+                out=oc[:, g, 4 * P * q:4 * P * (q + 1)].bitcast(FP8X4),
+                scales=osc[:, g, 4 * P * q:4 * P * (q + 1)],
+                in_=og_of[(q, g)][:].rearrange("p u o j -> p (u o j)"),
             )
 
         acc1_of = {}
@@ -229,21 +241,25 @@ def tile_mixerblock_pa_kernel(tc, x_proj, mix_mat, mix_b, out_w, out_b, out):
         mg_of = {}
 
         def mix_exit(half, b, g):
-            mg = mgp.tile([P, HALF, 4], BF16, name="mg", align_bytes=64)
-            mg_of[(half, b, g)] = mg
+            if half == 1 or g == 0:
+                mg = mgp.tile([P, 2 - half, HALF, 4], BF16, name="mg", align_bytes=64)
+                mg_of[(half, b, g)] = mg
+                if half == 0:
+                    mg_of[(0, b, 1)] = mg
             for jl in range(2):
                 nc.vector.tensor_tensor(
-                    out=mg[:, P * jl:P * (jl + 1), :],
+                    out=mg_of[(half, b, g)][:, g * (1 - half), P * jl:P * (jl + 1), :],
                     in0=acc1_of[(half, b, g, jl)][:].rearrange("p j s -> p s j"),
                     in1=bT[:, half, g, P * jl:P * (jl + 1), :],
                     op=ALU.add,
                 )
 
         def mix_quant(half, b, g):
+            lo, hi = (HALF * g, HALF * (g + 1)) if half == 1 else (0, 2 * HALF)
             nc.vector.quantize_mx(
-                out=mc[:, half, b, HALF * g:HALF * (g + 1)].bitcast(FP8X4),
-                scales=ms[:, half, b, HALF * g:HALF * (g + 1)],
-                in_=mg_of[(half, b, g)][:].rearrange("p s j -> p (s j)"),
+                out=mc[:, half, b, lo:hi].bitcast(FP8X4),
+                scales=ms[:, half, b, lo:hi],
+                in_=mg_of[(half, b, g)][:].rearrange("p g s j -> p (g s j)"),
             )
 
         acc2_of = {}
@@ -316,7 +332,6 @@ def tile_mixerblock_pa_kernel(tc, x_proj, mix_mat, mix_b, out_w, out_b, out):
         w_quant(5, 0)
         w_regroup(v, 6, 0)
         w_regroup(s, 7, 0)
-        mix_quant(0, 0, 0)
         w_quant(6, 0)
         w_quant(7, 0)
         mix_mm(0, 0, 1)
@@ -343,23 +358,19 @@ def tile_mixerblock_pa_kernel(tc, x_proj, mix_mat, mix_b, out_w, out_b, out):
         mix_mm(0, 1, 1)
         ow_exit(2, 0)
         ow_exit(2, 1)
-        mix_quant(0, 1, 0)
-        ow_quant(1, 0)
-        ow_quant(1, 1)
         ow_exit(3, 0)
         ow_exit(3, 1)
-        mix_exit(0, 1, 1)
-        ow_quant(2, 0)
-        ow_quant(2, 1)
-        mix_quant(0, 1, 1)
-        nc.vector.tensor_copy(out=outb[:], in_=outb16[:])
         w_mask(0, 1)
-        ow_quant(3, 0)
-        ow_quant(3, 1)
+        mix_exit(0, 1, 1)
+        nc.vector.tensor_copy(out=outb[:], in_=outb16[:])
+        ow_quant(1, 0)
+        mix_quant(0, 1, 1)
+        ow_quant(1, 1)
         x_regroup(2, 0)
         w_regroup(v, 0, 1)
         project(0, 0)
         w_regroup(v, 1, 1)
+        load_w(3, 1)
         w_quant(0, 1)
         w_mask(1, 1)
         x_regroup(2, 1)
@@ -374,7 +385,6 @@ def tile_mixerblock_pa_kernel(tc, x_proj, mix_mat, mix_b, out_w, out_b, out):
         mix_mm(0, 2, 1)
         w_regroup(s, 3, 1)
         w_mask(2, 1)
-        mix_quant(0, 2, 0)
         w_regroup(v, 4, 1)
         mix_exit(0, 2, 1)
         w_quant(3, 1)
@@ -412,7 +422,6 @@ def tile_mixerblock_pa_kernel(tc, x_proj, mix_mat, mix_b, out_w, out_b, out):
         x_quant(3, 1)
         mix_mm(1, 2, 1)
         project(1, 1)
-        mix_quant(0, 3, 0)
         mix_exit(1, 2, 1)
         mix_mm(0, 3, 1)
         mix_quant(1, 2, 1)

@@ -15,8 +15,10 @@ ACT = mybir.ActivationFunctionType
 P = 128
 B, S, E, H = 4, 512, 1024, 16
 FLOPS = 2 * B * E * S * S + 2 * B * S * E * E
-HC = 4
+HC = 2
 NCK = H // HC
+NRAW = 6
+SLOT = HC * S
 PAIRW = 192
 HALF = 256
 OB = E // P
@@ -34,35 +36,29 @@ def tile_mixerblock_pa_kernel(tc, x_proj, mix_mat, mix_b, out_w, out_b, out):
     with ExitStack() as ctx:
         keep = ctx.enter_context(tc.tile_pool(name="keep", bufs=1))
         rot = ctx.enter_context(tc.tile_pool(name="rot", bufs=5))
+        xcp = ctx.enter_context(tc.tile_pool(name="xcp", bufs=2))
         xgp = ctx.enter_context(tc.tile_pool(name="xgp", bufs=2))
-        g1p = ctx.enter_context(tc.tile_pool(name="g1p", bufs=2))
+        gvp = ctx.enter_context(tc.tile_pool(name="gvp", bufs=2))
         ogp = ctx.enter_context(tc.tile_pool(name="ogp", bufs=2))
         mgp = ctx.enter_context(tc.tile_pool(name="mgp", bufs=3))
+        mcp = ctx.enter_context(tc.tile_pool(name="mcp", bufs=2))
         ps1p = ctx.enter_context(tc.psum_pool(name="ps1p", bufs=4))
         ps2p = ctx.enter_context(tc.psum_pool(name="ps2p", bufs=4))
+        ctx.enter_context(tc.manual_schedule())
 
         xraw = {}
         owraw = {}
-        xc = [keep.tile([P, 8 * PAIRW], U32, name="xc%d" % b, align_bytes=64) for b in range(B)]
-        xs = [keep.tile([P, 8 * PAIRW], U8, name="xs%d" % b, align_bytes=64) for b in range(B)]
-        w0raw = [keep.tile([P, 2 * HC * HALF + 2 * P], BF16, name="w0raw%d" % k) for k in range(NCK)]
-        w1buf = [keep.tile([P, 4 * HC * HALF + 2 * P], BF16, name="w1raw%d" % k) for k in range(3)]
-        w1raw = [w1buf[k % 3] for k in range(NCK)]
-
-        def slots(k, half):
-            return (w0raw, w1raw)[half][k][:, 0:(2 + 2 * half) * HC * HALF].rearrange(
-                "p (j h s) -> p j h s", h=HC, s=HALF)
-
-        g0 = [keep.tile([P, 2 * HALF, 4], BF16, name="g0_%d" % k, align_bytes=64) for k in range(2)]
-        wc = keep.tile([P, 2, H * HALF], U32, name="wc", align_bytes=64)
-        ws = keep.tile([P, 2, H * HALF], U8, name="ws", align_bytes=64)
+        xc = [keep.tile([P, 8 * PAIRW], U32, name="xc%d" % b, align_bytes=64) for b in range(2)]
+        xs = [keep.tile([P, 8 * PAIRW], U8, name="xs%d" % b, align_bytes=64) for b in range(2)]
+        raw = [keep.tile([P, 4 * (SLOT + P)], BF16, name="raw%d" % k) for k in range(NRAW)]
+        gs = [keep.tile([P, S, 4], BF16, name="gs%d" % k, align_bytes=64) for k in range(2)]
+        wc = keep.tile([P, H * S], U32, name="wc", align_bytes=64)
+        ws = keep.tile([P, H * S], U8, name="ws", align_bytes=64)
         oc = keep.tile([P, 2, E], U32, name="oc", align_bytes=64)
         osc = keep.tile([P, 2, E], U8, name="osc", align_bytes=64)
-        mc = keep.tile([P, 2, B, 2 * HALF], U32, name="mc", align_bytes=64)
-        ms = keep.tile([P, 2, B, 2 * HALF], U8, name="ms", align_bytes=64)
-        bT = keep.tile([P, 2, 2, HALF, 4], BF16, name="bT")
-        mb = ogp.tile([P, S], BF16, name="mb", tag="og", align_bytes=64)
-        sel = ogp.tile([P, H, E // H], BF16, name="sel", tag="og", align_bytes=64)
+        bT = keep.tile([P, 2, S, 4], BF16, name="bT")
+        mb = keep.tile([P, S], BF16, name="mb")
+        sel = keep.tile([P, H, E // H], BF16, name="sel")
         ident = keep.tile([P, P], BF16, name="ident")
         mask = keep.tile([P, P], BF16, name="mask")
         outb16 = keep.tile([P, OB], BF16, name="outb16")
@@ -70,34 +66,25 @@ def tile_mixerblock_pa_kernel(tc, x_proj, mix_mat, mix_b, out_w, out_b, out):
 
         def load_x(b):
             xraw[b] = rot.tile([P, 4, E], BF16, name="xraw", tag="rot")
-            nc.sync.dma_start(out=xraw[b][:], in_=x_proj[b].rearrange("(j p) c -> p j c", p=P))
+            for lo, hi in ([(0, 576), (576, E)] if b == 0 else [(0, E)]):
+                nc.sync.dma_start(
+                    out=xraw[b][:, :, lo:hi], in_=x_proj[b][:, lo:hi].rearrange("(j p) c -> p j c", p=P))
 
         def load_ow(q):
             owraw[q] = rot.tile([P, 4, E], BF16, name="owraw", tag="rot")
             nc.sync.dma_start(
                 out=owraw[q][:], in_=out_w.rearrange("(p ob) c -> p ob c", ob=OB)[:, 4 * q:4 * q + 4, :])
 
-        def load_w(k, half):
-            raw = slots(k, half)
-            last = 1 if half == 0 else 3
-            for j in range(last + 1):
-                lo = P if j == last else 0
+        def slots(k):
+            return raw[k % NRAW][:, 0:4 * SLOT].rearrange("p (j h s) -> p j h s", h=HC, s=S)
+
+        def load_w(k):
+            for j in range(4):
                 nc.sync.dma_start(
-                    out=raw[:, j, :, lo:HALF],
-                    in_=mix_mat[HC * k:HC * (k + 1), P * j:P * (j + 1),
-                                HALF * half + lo:HALF * (half + 1)].rearrange("h p s -> p h s"),
+                    out=slots(k)[:, j, :, P * j:S],
+                    in_=mix_mat[HC * k:HC * (k + 1), P * j:P * (j + 1), P * j:S].rearrange("h p s -> p h s"),
                 )
 
-        def spread_b(half, g):
-            pb = ps2p.tile([P, 4, HALF], BF16, name="pb", tag="ps2")
-            for j in range(4):
-                i = 4 * g + j
-                nc.tensor.matmul(
-                    pb[:, j, :], lhsT=sel[:, 2 * i:2 * i + 2, :].rearrange("p h e -> p (h e)"),
-                    rhs=mb[:, HALF * half:HALF * (half + 1)], start=True, stop=True)
-            nc.scalar.copy(out=bT[:, half, g, :, :], in_=pb[:].rearrange("p j s -> p s j"))
-
-        ctx.enter_context(tc.manual_schedule())
         make_identity(nc, ident[:])
         nc.gpsimd.memset(mask[:], 1.0)
         nc.gpsimd.affine_select(
@@ -105,44 +92,52 @@ def tile_mixerblock_pa_kernel(tc, x_proj, mix_mat, mix_b, out_w, out_b, out):
             fill=0.0, base=0, channel_multiplier=-1,
         )
 
+        def zero_raw(eng, k):
+            for j in range(1, 4):
+                eng.memset(slots(k)[:, j, :, 0:P * j].bitcast(I32), 0)
+
         def zero_x(eng, b):
             eng.memset(
                 xc[b][:].bitcast(I32).rearrange("p (i w) -> p i w", w=PAIRW)[:, :, 64:128], 0)
             eng.memset(
                 xs[b][:].bitcast(I32).rearrange("p (i w) -> p i w", w=PAIRW // 4)[:, :, 16:32], 0)
 
-        def zero_w(eng, half):
-            for k in range(3 if half else NCK):
-                eng.memset(slots(k, half)[:, 2 * half + 1, :, 0:P].bitcast(I32), 0)
-
         nc.vector.memset(mb[:].bitcast(I32), 0)
-        zero_w(nc.vector, 0)
-        zero_x(nc.gpsimd, 1)
-        zero_w(nc.gpsimd, 1)
-        zero_x(nc.gpsimd, 2)
-        zero_x(nc.gpsimd, 3)
+        zero_raw(nc.vector, 0)
         nc.vector.tensor_copy(out=sel[:], in_=ident[:, 0:H].unsqueeze(2).to_broadcast([P, H, E // H]))
         for k in range(2):
-            nc.vector.memset(g0[k][:].rearrange("p s t -> p (s t)").bitcast(I32).rearrange("p (s w) -> p s w", w=2)[:, :, 1:2], 0)
-        zero_x(nc.vector, 0)
+            nc.vector.memset(
+                gs[k][:, 0:HALF, :].rearrange("p s t -> p (s t)").bitcast(I32).rearrange(
+                    "p (s w) -> p s w", w=2)[:, :, 1:2], 0)
+        zero_raw(nc.gpsimd, 1)
+        zero_raw(nc.gpsimd, 2)
+        zero_x(nc.gpsimd, 0)
+        for k in range(3, NRAW):
+            zero_raw(nc.gpsimd, k)
+        zero_x(nc.gpsimd, 1)
 
         nc.sync.dma_start(out=mb[0:H, :], in_=mix_b)
-        load_w(0, 0)
+        load_w(0)
+        load_w(1)
+        load_w(2)
         load_x(0)
-        load_w(1, 0)
-        load_w(2, 0)
-        load_w(3, 0)
-        load_x(1)
+        load_w(3)
+        load_w(4)
         load_ow(0)
+        load_w(5)
         load_ow(1)
-        load_x(2)
         nc.sync.dma_start(out=outb16[:], in_=out_b.rearrange("(p ob) -> p ob", ob=OB))
-        for k in range(3):
-            load_w(k, 1)
-        load_x(3)
+
+        def spread_b(eng_copy, half, g):
+            pb = ps2p.tile([P, 4, HALF], BF16, name="pb", tag="ps2")
+            for j in range(4):
+                i = 4 * g + j
+                nc.tensor.matmul(
+                    pb[:, j, :], lhsT=sel[:, 2 * i:2 * i + 2, :].rearrange("p h e -> p (h e)"),
+                    rhs=mb[:, HALF * half:HALF * (half + 1)], start=True, stop=True)
+            eng_copy(out=bT[:, g, HALF * half:HALF * (half + 1), :], in_=pb[:].rearrange("p j s -> p s j"))
 
         xg_of = {}
-
         XCUT = (0, 576, 1024)
 
         def x_regroup(b, ch):
@@ -159,38 +154,39 @@ def tile_mixerblock_pa_kernel(tc, x_proj, mix_mat, mix_b, out_w, out_b, out):
                 c1 = min(c0 + P if c0 % P else c0 + 64, hi)
                 w0 = PAIRW * (c0 // P) + (P if c0 % P else 0)
                 nc.vector.quantize_mx(
-                    out=xc[b][:, w0:w0 + c1 - c0].bitcast(FP8X4),
-                    scales=xs[b][:, w0:w0 + c1 - c0],
+                    out=xc[b % 2][:, w0:w0 + c1 - c0].bitcast(FP8X4),
+                    scales=xs[b % 2][:, w0:w0 + c1 - c0],
                     in_=flat[:, 4 * (c0 - lo):4 * (c1 - lo)],
                 )
                 c0 = c1
 
-        def w_mask(k, half):
-            step = HC * HALF + P
-            lo = 2 * half * HC * HALF
-            d = (w0raw, w1raw)[half][k][:, lo:lo + 2 * step].rearrange("p (j x) -> p j x", x=step)
-            d = d[:, :, 0:HC * HALF].rearrange("p j (h s) -> p j h s", s=HALF)[:, :, :, 0:P]
+        def w_mask(k):
+            d = raw[k % NRAW][:].rearrange("p (j x) -> p j x", x=SLOT + P)
+            d = d[:, :, 0:SLOT].rearrange("p j (h s) -> p j h s", s=S)[:, :, :, 0:P]
             nc.vector.tensor_tensor(
-                out=d, in0=d, in1=mask[:].unsqueeze(1).unsqueeze(1).to_broadcast([P, 2, HC, P]), op=ALU.mult)
+                out=d, in0=d, in1=mask[:].unsqueeze(1).unsqueeze(1).to_broadcast([P, 4, HC, P]), op=ALU.mult)
 
         g_of = {}
 
-        def w_regroup(eng_copy, hp, half):
-            k, r = divmod(2 * hp, HC)
-            if half == 1:
-                g = g1p.tile([P, 2 * HALF, 4], BF16, name="g1", align_bytes=64)
-                regroup(eng_copy, g[:], slots(k, 1)[:, :, r:r + 2, :].rearrange("p t h s -> p t (h s)"))
-            else:
-                g = g0[hp % 2]
-                regroup(eng_copy, g[:, :, 0:2], slots(k, 0)[:, :, r:r + 2, :].rearrange("p t h s -> p t (h s)"))
-            g_of[(hp, half)] = g
+        def w_regroup_v(h):
+            g = gvp.tile([P, S, 4], BF16, name="gv", align_bytes=64)
+            g_of[h] = g
+            regroup(nc.vector.tensor_copy, g[:], slots(h // HC)[:, :, h % HC, :])
 
-        def w_quant(hp, half):
-            w0 = 2 * hp * HALF
+        on_scalar = []
+
+        def w_regroup_s(h):
+            g = gs[len(on_scalar) % 2]
+            on_scalar.append(h)
+            g_of[h] = g
+            regroup(nc.scalar.copy, g[:, 0:HALF, 0:2], slots(h // HC)[:, 0:2, h % HC, 0:HALF])
+            regroup(nc.scalar.copy, g[:, HALF:S, :], slots(h // HC)[:, :, h % HC, HALF:S])
+
+        def w_quant(h):
             nc.vector.quantize_mx(
-                out=wc[:, half, w0:w0 + 2 * HALF].bitcast(FP8X4),
-                scales=ws[:, half, w0:w0 + 2 * HALF],
-                in_=g_of[(hp, half)][:].rearrange("p s t -> p (s t)"),
+                out=wc[:, h * S:(h + 1) * S].bitcast(FP8X4),
+                scales=ws[:, h * S:(h + 1) * S],
+                in_=g_of[h][:].rearrange("p s t -> p (s t)"),
             )
 
         pt_of = {}
@@ -218,221 +214,180 @@ def tile_mixerblock_pa_kernel(tc, x_proj, mix_mat, mix_b, out_w, out_b, out):
             )
 
         acc1_of = {}
+        mg_of = {}
+        mc_of = {}
+        ms_of = {}
 
-        def mix_mm(half, b, g):
-            for jl in range(2):
+        def mix_mm(b, g):
+            for q in range(4):
                 acc = ps1p.tile([P, 4, P], F32, name="acc1")
-                acc1_of[(half, b, g, jl)] = acc
+                acc1_of[(b, g, q)] = acc
                 for j in range(4):
                     i = 4 * g + j
                     for h2 in range(2):
                         x0 = PAIRW * i + 64 * h2
-                        w0 = (2 * i + h2) * HALF + P * jl
+                        w0 = (2 * i + h2) * S + P * q
                         nc.tensor.matmul_mx(
                             out=acc[:, j, :],
-                            lhsT=xc[b][:, x0:x0 + P].bitcast(FP8X4),
-                            lhsT_scale=xs[b][:, x0:x0 + P],
-                            rhs=wc[:, half, w0:w0 + P].bitcast(FP8X4),
-                            rhs_scale=ws[:, half, w0:w0 + P],
+                            lhsT=xc[b % 2][:, x0:x0 + P].bitcast(FP8X4),
+                            lhsT_scale=xs[b % 2][:, x0:x0 + P],
+                            rhs=wc[:, w0:w0 + P].bitcast(FP8X4),
+                            rhs_scale=ws[:, w0:w0 + P],
                             start=(h2 == 0),
                             stop=(h2 == 1),
                         )
 
-        mg_of = {}
-
-        def mix_exit(half, b, g):
-            if half == 1 or g == 0:
-                mg = mgp.tile([P, 2 - half, HALF, 4], BF16, name="mg", align_bytes=64)
-                mg_of[(half, b, g)] = mg
-                if half == 0:
-                    mg_of[(0, b, 1)] = mg
-            for jl in range(2):
+        def mix_exit(b, g, qs=range(4)):
+            for q in qs:
+                if q == 0:
+                    mg_of[(b, g)] = mgp.tile([P, S, 4], BF16, name="mg", align_bytes=64)
                 nc.vector.tensor_tensor(
-                    out=mg_of[(half, b, g)][:, g * (1 - half), P * jl:P * (jl + 1), :],
-                    in0=acc1_of[(half, b, g, jl)][:].rearrange("p j s -> p s j"),
-                    in1=bT[:, half, g, P * jl:P * (jl + 1), :],
+                    out=mg_of[(b, g)][:, P * q:P * (q + 1), :],
+                    in0=acc1_of[(b, g, q)][:].rearrange("p j s -> p s j"),
+                    in1=bT[:, g, P * q:P * (q + 1), :],
                     op=ALU.add,
                 )
 
-        def mix_quant(half, b, g):
-            lo, hi = (HALF * g, HALF * (g + 1)) if half == 1 else (0, 2 * HALF)
+        def mix_quant(b, g):
+            if g == 0:
+                mc_of[b] = mcp.tile([P, 2, S], U32, name="mc", align_bytes=64)
+                ms_of[b] = mcp.tile([P, 2, S], U8, name="ms", align_bytes=64)
             nc.vector.quantize_mx(
-                out=mc[:, half, b, lo:hi].bitcast(FP8X4),
-                scales=ms[:, half, b, lo:hi],
-                in_=mg_of[(half, b, g)][:].rearrange("p g s j -> p (g s j)"),
+                out=mc_of[b][:, g, :].bitcast(FP8X4),
+                scales=ms_of[b][:, g, :],
+                in_=mg_of[(b, g)][:].rearrange("p s j -> p (s j)"),
             )
-
-        acc2_of = {}
-
-        def out_mm(half, b, obp):
-            acc = ps2p.tile([P, 2, HALF], F32, name="acc2", tag="ps2")
-            acc2_of[(half, b, obp)] = acc
-            for u in range(2):
-                ob = 2 * obp + u
-                for g in range(2):
-                    nc.tensor.matmul_mx(
-                        out=acc[:, u, :],
-                        lhsT=oc[:, g, P * ob:P * (ob + 1)].bitcast(FP8X4),
-                        lhsT_scale=osc[:, g, P * ob:P * (ob + 1)],
-                        rhs=mc[:, half, b, HALF * g:HALF * (g + 1)].bitcast(FP8X4),
-                        rhs_scale=ms[:, half, b, HALF * g:HALF * (g + 1)],
-                        start=(g == 0),
-                        stop=(g == 1),
-                    )
 
         ot_of = {}
 
-        def out_exit(half, b, obp, both):
-            if obp == 0:
-                ot_of[0] = rot.tile([P, OB, HALF], F32, name="ot8", tag="rot")
-            acc = acc2_of[(half, b, obp)]
-            for u in range(2):
-                ob = 2 * obp + u
-                ot = ot_of[0][:, ob, :]
-                if both and u == 1:
-                    nc.vector.tensor_scalar(out=ot, in0=acc[:, u, :], scalar1=outb[:, ob:ob + 1], scalar2=None, op0=ALU.add)
+        def project(b, obs, on_vector=()):
+            for ob in obs:
+                acc = ps2p.tile([P, S], F32, name="acc2", tag="ps2")
+                for g in range(2):
+                    nc.tensor.matmul_mx(
+                        out=acc[:],
+                        lhsT=oc[:, g, P * ob:P * (ob + 1)].bitcast(FP8X4),
+                        lhsT_scale=osc[:, g, P * ob:P * (ob + 1)],
+                        rhs=mc_of[b][:, g, :].bitcast(FP8X4),
+                        rhs_scale=ms_of[b][:, g, :],
+                        start=(g == 0),
+                        stop=(g == 1),
+                    )
+                if ob % 4 == 0:
+                    ot_of[0] = rot.tile([P, 4, S], F32, name="ot4", tag="rot")
+                ot = ot_of[0][:, ob % 4, :]
+                if ob in on_vector:
+                    nc.vector.tensor_scalar(out=ot, in0=acc[:], scalar1=outb[:, ob:ob + 1], scalar2=None, op0=ALU.add)
                 else:
-                    nc.scalar.activation(out=ot, in_=acc[:, u, :], func=ACT.Identity, bias=outb[:, ob:ob + 1], scale=1.0)
-            nc.sync.dma_start(
-                out=out[b].rearrange("(p ob) s -> p ob s", ob=OB)[:, 2 * obp:2 * obp + 2, HALF * half:HALF * (half + 1)],
-                in_=ot_of[0][:, 2 * obp:2 * obp + 2, :],
-            )
+                    nc.scalar.activation(out=ot, in_=acc[:], func=ACT.Identity, bias=outb[:, ob:ob + 1], scale=1.0)
+                if ob % 2 == 1:
+                    nc.sync.dma_start(
+                        out=out[b].rearrange("(p ob) s -> p ob s", ob=OB)[:, ob - 1:ob + 1, :],
+                        in_=ot_of[0][:, ob % 4 - 1:ob % 4 + 1, :],
+                    )
 
         v, s = nc.vector.tensor_copy, nc.scalar.copy
-
-        def project(half, b, both=False):
-            for obp in range(4):
-                out_mm(half, b, obp)
-                out_exit(half, b, obp, both)
-
-        for half in range(2):
-            for g in range(2):
-                spread_b(half, g)
-        w_mask(0, 0)
-        w_regroup(v, 0, 0)
-        w_regroup(s, 1, 0)
+        spread_b(s, 0, 0)
+        spread_b(s, 1, 0)
+        w_mask(0)
+        w_regroup_v(0)
+        w_regroup_s(1)
+        w_mask(1)
+        w_quant(0)
+        w_regroup_v(2)
+        load_w(6)
+        w_regroup_s(3)
+        w_quant(1)
+        w_mask(2)
+        w_quant(2)
+        w_regroup_v(4)
+        load_w(7)
+        w_regroup_s(5)
+        w_quant(3)
         x_regroup(0, 0)
-        w_quant(0, 0)
-        w_mask(1, 0)
-        w_regroup(v, 2, 0)
-        w_quant(1, 0)
-        w_regroup(s, 3, 0)
-        x_regroup(0, 1)
-        w_quant(2, 0)
+        w_quant(4)
+        w_mask(3)
+        w_quant(5)
+        w_regroup_v(6)
+        w_regroup_s(7)
         x_quant(0, 0)
-        w_mask(2, 0)
-        w_quant(3, 0)
-        mix_mm(0, 0, 0)
-        w_regroup(v, 4, 0)
-        w_regroup(s, 5, 0)
-        w_mask(3, 0)
-        w_quant(4, 0)
-        mix_exit(0, 0, 0)
+        x_regroup(0, 1)
+        load_x(1)
+        w_quant(6)
+        w_mask(4)
+        w_quant(7)
+        w_regroup_v(8)
+        mix_mm(0, 0)
+        w_regroup_s(9)
         x_quant(0, 1)
-        w_quant(5, 0)
-        w_regroup(v, 6, 0)
-        w_regroup(s, 7, 0)
-        w_quant(6, 0)
-        w_quant(7, 0)
-        mix_mm(0, 0, 1)
-        x_regroup(1, 0)
-        x_regroup(1, 1)
+        spread_b(s, 0, 1)
+        spread_b(s, 1, 1)
+        w_quant(8)
+        w_mask(5)
+        mix_exit(0, 0, (0, 1))
+        w_regroup_s(11)
+        w_quant(9)
+        w_regroup_v(10)
+        mix_exit(0, 0, (2, 3))
         for obp in range(2):
             for g in range(2):
                 ow_transpose(obp, g)
-        mix_exit(0, 0, 1)
-        x_quant(1, 0)
-        mix_mm(0, 1, 0)
-        mix_quant(0, 0, 1)
+        load_x(2)
+        w_mask(6)
+        w_quant(10)
+        w_quant(11)
         ow_exit(0, 0)
-        ow_exit(0, 1)
-        x_quant(1, 1)
         ow_exit(1, 0)
+        w_regroup_s(12)
+        mix_quant(0, 0)
+        w_regroup_s(13)
+        w_mask(7)
+        ow_exit(0, 1)
         ow_exit(1, 1)
+        ow_quant(0, 0)
+        w_regroup_v(14)
+        w_quant(12)
+        w_regroup_s(15)
+        w_quant(13)
+        ow_quant(0, 1)
+        w_quant(14)
         for obp in range(2, 4):
             for g in range(2):
                 ow_transpose(obp, g)
-        mix_exit(0, 1, 0)
-        ow_quant(0, 0)
-        ow_quant(0, 1)
-        mix_mm(0, 1, 1)
         ow_exit(2, 0)
-        ow_exit(2, 1)
         ow_exit(3, 0)
+        w_quant(15)
+        mix_mm(0, 1)
+        ow_exit(2, 1)
         ow_exit(3, 1)
-        w_mask(0, 1)
-        mix_exit(0, 1, 1)
         nc.vector.tensor_copy(out=outb[:], in_=outb16[:])
         ow_quant(1, 0)
-        mix_quant(0, 1, 1)
+        x_regroup(1, 0)
+        mix_exit(0, 1, (0, 1))
         ow_quant(1, 1)
+        mix_exit(0, 1, (2, 3))
+        x_regroup(1, 1)
+        x_quant(1, 0)
+        mix_quant(0, 1)
+        mix_mm(1, 0)
+        x_quant(1, 1)
         x_regroup(2, 0)
-        w_regroup(v, 0, 1)
-        project(0, 0)
-        w_regroup(v, 1, 1)
-        load_w(3, 1)
-        w_quant(0, 1)
-        w_mask(1, 1)
-        x_regroup(2, 1)
-        x_quant(2, 0)
-        w_quant(1, 1)
-        mix_mm(0, 2, 0)
-        project(0, 1)
-        w_regroup(v, 2, 1)
-        x_quant(2, 1)
-        mix_exit(0, 2, 0)
-        w_quant(2, 1)
-        mix_mm(0, 2, 1)
-        w_regroup(s, 3, 1)
-        w_mask(2, 1)
-        w_regroup(v, 4, 1)
-        mix_exit(0, 2, 1)
-        w_quant(3, 1)
-        mix_mm(1, 0, 0)
-        mix_mm(1, 1, 0)
-        mix_quant(0, 2, 1)
-        w_regroup(s, 5, 1)
-        w_quant(4, 1)
-        w_mask(3, 1)
-        mix_exit(1, 0, 0)
-        project(0, 2)
-        w_regroup(v, 6, 1)
-        mix_quant(1, 0, 0)
-        mix_exit(1, 1, 0)
-        mix_mm(1, 2, 0)
-        w_regroup(s, 7, 1)
-        w_quant(5, 1)
-        mix_quant(1, 1, 0)
-        w_quant(6, 1)
-        mix_exit(1, 2, 0)
-        x_regroup(3, 0)
-        w_quant(7, 1)
-        mix_mm(1, 0, 1)
-        mix_quant(1, 2, 0)
-        mix_mm(1, 1, 1)
-        mix_exit(1, 0, 1)
-        x_quant(3, 0)
-        mix_quant(1, 0, 1)
-        mix_exit(1, 1, 1)
-        x_regroup(3, 1)
-        mix_mm(0, 3, 0)
-        project(1, 0)
-        mix_quant(1, 1, 1)
-        mix_exit(0, 3, 0)
-        x_quant(3, 1)
-        mix_mm(1, 2, 1)
-        project(1, 1)
-        mix_exit(1, 2, 1)
-        mix_mm(0, 3, 1)
-        mix_quant(1, 2, 1)
-        mix_exit(0, 3, 1)
-        mix_mm(1, 3, 0)
-        project(1, 2)
-        mix_quant(0, 3, 1)
-        mix_exit(1, 3, 0)
-        mix_mm(1, 3, 1)
-        mix_quant(1, 3, 0)
-        project(0, 3)
-        mix_exit(1, 3, 1)
-        mix_quant(1, 3, 1)
-        project(1, 3, True)
+        load_x(3)
+        for b in range(1, B):
+            project(b - 1, range(4))
+            mix_exit(b, 0)
+            mix_mm(b, 1)
+            if b + 1 < B:
+                x_quant(b + 1, 0)
+            if b + 1 < B:
+                x_regroup(b + 1, 1)
+            project(b - 1, range(4, 8))
+            mix_quant(b, 0)
+            mix_exit(b, 1)
+            if b + 1 < B:
+                mix_mm(b + 1, 0)
+                x_quant(b + 1, 1)
+            if b + 2 < B:
+                x_regroup(b + 2, 0)
+            mix_quant(b, 1)
+        project(B - 1, range(OB), (0, 2, 4, 6))

@@ -38,7 +38,6 @@ def tile_mixerblock_pa_kernel(tc, x_proj, mix_mat, mix_b, out_w, out_b, out):
         rot = ctx.enter_context(tc.tile_pool(name="rot", bufs=5))
         xcp = ctx.enter_context(tc.tile_pool(name="xcp", bufs=2))
         xgp = ctx.enter_context(tc.tile_pool(name="xgp", bufs=2))
-        gvp = ctx.enter_context(tc.tile_pool(name="gvp", bufs=2))
         ogp = ctx.enter_context(tc.tile_pool(name="ogp", bufs=2))
         mgp = ctx.enter_context(tc.tile_pool(name="mgp", bufs=3))
         mcp = ctx.enter_context(tc.tile_pool(name="mcp", bufs=2))
@@ -51,7 +50,7 @@ def tile_mixerblock_pa_kernel(tc, x_proj, mix_mat, mix_b, out_w, out_b, out):
         xc = [keep.tile([P, 8 * PAIRW], U32, name="xc%d" % b, align_bytes=64) for b in range(2)]
         xs = [keep.tile([P, 8 * PAIRW], U8, name="xs%d" % b, align_bytes=64) for b in range(2)]
         raw = [keep.tile([P, 4 * (SLOT + P)], BF16, name="raw%d" % k) for k in range(NRAW)]
-        gs = [keep.tile([P, S, 4], BF16, name="gs%d" % k, align_bytes=64) for k in range(2)]
+        gt = [keep.tile([P, S, 4], BF16, name="gt%d" % k, align_bytes=64) for k in range(4)]
         wc = keep.tile([P, H * S], U32, name="wc", align_bytes=64)
         ws = keep.tile([P, H * S], U8, name="ws", align_bytes=64)
         oc = keep.tile([P, 2, E], U32, name="oc", align_bytes=64)
@@ -78,11 +77,11 @@ def tile_mixerblock_pa_kernel(tc, x_proj, mix_mat, mix_b, out_w, out_b, out):
         def slots(k):
             return raw[k % NRAW][:, 0:4 * SLOT].rearrange("p (j h s) -> p j h s", h=HC, s=S)
 
-        def load_w(k):
+        def load_w(k, h0=0, h1=HC):
             for j in range(4):
                 nc.sync.dma_start(
-                    out=slots(k)[:, j, :, P * j:S],
-                    in_=mix_mat[HC * k:HC * (k + 1), P * j:P * (j + 1), P * j:S].rearrange("h p s -> p h s"),
+                    out=slots(k)[:, j, h0:h1, P * j:S],
+                    in_=mix_mat[HC * k + h0:HC * k + h1, P * j:P * (j + 1), P * j:S].rearrange("h p s -> p h s"),
                 )
 
         make_identity(nc, ident[:])
@@ -93,8 +92,8 @@ def tile_mixerblock_pa_kernel(tc, x_proj, mix_mat, mix_b, out_w, out_b, out):
         )
 
         def zero_raw(eng, k):
-            for j in range(1, 4):
-                eng.memset(slots(k)[:, j, :, 0:P * j].bitcast(I32), 0)
+            for j in (1, 3):
+                eng.memset(slots(k)[:, j, :, P * (j - 1):P * j].bitcast(I32), 0)
 
         def zero_x(eng, b):
             eng.memset(
@@ -104,12 +103,12 @@ def tile_mixerblock_pa_kernel(tc, x_proj, mix_mat, mix_b, out_w, out_b, out):
 
         nc.vector.memset(mb[:].bitcast(I32), 0)
         zero_raw(nc.vector, 0)
+        zero_raw(nc.vector, 1)
         nc.vector.tensor_copy(out=sel[:], in_=ident[:, 0:H].unsqueeze(2).to_broadcast([P, H, E // H]))
-        for k in range(2):
+        for k in range(4):
             nc.vector.memset(
-                gs[k][:, 0:HALF, :].rearrange("p s t -> p (s t)").bitcast(I32).rearrange(
+                gt[k][:, 0:HALF, :].rearrange("p s t -> p (s t)").bitcast(I32).rearrange(
                     "p (s w) -> p s w", w=2)[:, :, 1:2], 0)
-        zero_raw(nc.gpsimd, 1)
         zero_raw(nc.gpsimd, 2)
         zero_x(nc.gpsimd, 0)
         for k in range(3, NRAW):
@@ -117,15 +116,15 @@ def tile_mixerblock_pa_kernel(tc, x_proj, mix_mat, mix_b, out_w, out_b, out):
         zero_x(nc.gpsimd, 1)
 
         nc.sync.dma_start(out=mb[0:H, :], in_=mix_b)
-        load_w(0)
+        for h in range(HC):
+            load_w(0, h, h + 1)
         load_w(1)
         load_w(2)
         load_x(0)
         load_w(3)
         load_w(4)
-        load_ow(0)
         load_w(5)
-        load_ow(1)
+        load_ow(0)
         nc.sync.dma_start(out=outb16[:], in_=out_b.rearrange("(p ob) -> p ob", ob=OB))
 
         def spread_b(eng_copy, half, g):
@@ -160,27 +159,29 @@ def tile_mixerblock_pa_kernel(tc, x_proj, mix_mat, mix_b, out_w, out_b, out):
                 )
                 c0 = c1
 
-        def w_mask(k):
+        def w_mask(k, h0=0, h1=HC):
             d = raw[k % NRAW][:].rearrange("p (j x) -> p j x", x=SLOT + P)
-            d = d[:, :, 0:SLOT].rearrange("p j (h s) -> p j h s", s=S)[:, :, :, 0:P]
+            d = d[:, :, 0:SLOT].rearrange("p j (h s) -> p j h s", s=S)[:, :, h0:h1, 0:P]
             nc.vector.tensor_tensor(
-                out=d, in0=d, in1=mask[:].unsqueeze(1).unsqueeze(1).to_broadcast([P, 4, HC, P]), op=ALU.mult)
+                out=d, in0=d, in1=mask[:].unsqueeze(1).unsqueeze(1).to_broadcast([P, 4, h1 - h0, P]), op=ALU.mult)
 
         g_of = {}
 
-        def w_regroup_v(h):
-            g = gvp.tile([P, S, 4], BF16, name="gv", align_bytes=64)
-            g_of[h] = g
-            regroup(nc.vector.tensor_copy, g[:], slots(h // HC)[:, :, h % HC, :])
+        done = {0: 0, 1: 0}
 
-        on_scalar = []
+        def w_regroup(h, who):
+            g = gt[2 * who + done[who] % 2]
+            done[who] += 1
+            g_of[h] = g
+            eng_copy = (nc.vector.tensor_copy, nc.scalar.copy)[who]
+            regroup(eng_copy, g[:, 0:HALF, 0:2], slots(h // HC)[:, 0:2, h % HC, 0:HALF])
+            regroup(eng_copy, g[:, HALF:S, :], slots(h // HC)[:, :, h % HC, HALF:S])
+
+        def w_regroup_v(h):
+            w_regroup(h, 0)
 
         def w_regroup_s(h):
-            g = gs[len(on_scalar) % 2]
-            on_scalar.append(h)
-            g_of[h] = g
-            regroup(nc.scalar.copy, g[:, 0:HALF, 0:2], slots(h // HC)[:, 0:2, h % HC, 0:HALF])
-            regroup(nc.scalar.copy, g[:, HALF:S, :], slots(h // HC)[:, :, h % HC, HALF:S])
+            w_regroup(h, 1)
 
         def w_quant(h):
             nc.vector.quantize_mx(
@@ -289,30 +290,34 @@ def tile_mixerblock_pa_kernel(tc, x_proj, mix_mat, mix_b, out_w, out_b, out):
         v, s = nc.vector.tensor_copy, nc.scalar.copy
         spread_b(s, 0, 0)
         spread_b(s, 1, 0)
-        w_mask(0)
-        w_regroup_v(0)
-        w_regroup_s(1)
+        w_mask(0, 0, 1)
+        w_regroup_s(0)
+        w_mask(0, 1, 2)
+        w_regroup_v(1)
         w_mask(1)
         w_quant(0)
-        w_regroup_v(2)
-        load_w(6)
         w_regroup_s(3)
+        w_regroup_v(2)
         w_quant(1)
+        load_w(6)
         w_mask(2)
+        w_regroup_s(5)
         w_quant(2)
+        w_quant(3)
         w_regroup_v(4)
         load_w(7)
-        w_regroup_s(5)
-        w_quant(3)
         x_regroup(0, 0)
-        w_quant(4)
         w_mask(3)
-        w_quant(5)
-        w_regroup_v(6)
         w_regroup_s(7)
+        w_quant(5)
+        w_quant(4)
+        w_regroup_v(6)
         x_quant(0, 0)
         x_regroup(0, 1)
+        spread_b(s, 0, 1)
+        spread_b(s, 1, 1)
         load_x(1)
+        load_ow(1)
         w_quant(6)
         w_mask(4)
         w_quant(7)
@@ -320,8 +325,6 @@ def tile_mixerblock_pa_kernel(tc, x_proj, mix_mat, mix_b, out_w, out_b, out):
         mix_mm(0, 0)
         w_regroup_s(9)
         x_quant(0, 1)
-        spread_b(s, 0, 1)
-        spread_b(s, 1, 1)
         w_quant(8)
         w_mask(5)
         mix_exit(0, 0, (0, 1))
@@ -338,7 +341,7 @@ def tile_mixerblock_pa_kernel(tc, x_proj, mix_mat, mix_b, out_w, out_b, out):
         w_quant(11)
         ow_exit(0, 0)
         ow_exit(1, 0)
-        w_regroup_s(12)
+        w_regroup_v(12)
         mix_quant(0, 0)
         w_regroup_s(13)
         w_mask(7)
@@ -351,6 +354,7 @@ def tile_mixerblock_pa_kernel(tc, x_proj, mix_mat, mix_b, out_w, out_b, out):
         w_quant(13)
         ow_quant(0, 1)
         w_quant(14)
+        x_regroup(1, 0)
         for obp in range(2, 4):
             for g in range(2):
                 ow_transpose(obp, g)
@@ -360,17 +364,16 @@ def tile_mixerblock_pa_kernel(tc, x_proj, mix_mat, mix_b, out_w, out_b, out):
         mix_mm(0, 1)
         ow_exit(2, 1)
         ow_exit(3, 1)
-        nc.vector.tensor_copy(out=outb[:], in_=outb16[:])
+        x_quant(1, 0)
         ow_quant(1, 0)
-        x_regroup(1, 0)
+        nc.vector.tensor_copy(out=outb[:], in_=outb16[:])
         mix_exit(0, 1, (0, 1))
+        x_regroup(1, 1)
         ow_quant(1, 1)
         mix_exit(0, 1, (2, 3))
-        x_regroup(1, 1)
-        x_quant(1, 0)
-        mix_quant(0, 1)
         mix_mm(1, 0)
         x_quant(1, 1)
+        mix_quant(0, 1)
         x_regroup(2, 0)
         load_x(3)
         for b in range(1, B):

@@ -63,11 +63,12 @@ def tile_mixerblock_pa_kernel(tc, x_proj, mix_mat, mix_b, out_w, out_b, out):
         outb16 = keep.tile([P, OB], BF16, name="outb16")
         outb = keep.tile([P, OB], F32, name="outb")
 
-        def load_x(b):
-            xraw[b] = rot.tile([P, 4, E], BF16, name="xraw", tag="rot")
-            for lo, hi in ([(0, 576), (576, E)] if b == 0 else [(0, E)]):
-                nc.sync.dma_start(
-                    out=xraw[b][:, :, lo:hi], in_=x_proj[b][:, lo:hi].rearrange("(j p) c -> p j c", p=P))
+        def load_x(b, cols=(0, E)):
+            if b not in xraw:
+                xraw[b] = rot.tile([P, 4, E], BF16, name="xraw", tag="rot")
+            lo, hi = cols
+            nc.sync.dma_start(
+                out=xraw[b][:, :, lo:hi], in_=x_proj[b][:, lo:hi].rearrange("(j p) c -> p j c", p=P))
 
         def load_ow(q):
             owraw[q] = rot.tile([P, 4, E], BF16, name="owraw", tag="rot")
@@ -103,25 +104,22 @@ def tile_mixerblock_pa_kernel(tc, x_proj, mix_mat, mix_b, out_w, out_b, out):
 
         nc.vector.memset(mb[:].bitcast(I32), 0)
         zero_raw(nc.vector, 0)
-        zero_raw(nc.vector, 1)
-        nc.vector.tensor_copy(out=sel[:], in_=ident[:, 0:H].unsqueeze(2).to_broadcast([P, H, E // H]))
         for k in range(4):
             nc.vector.memset(
                 gt[k][:, 0:HALF, :].rearrange("p s t -> p (s t)").bitcast(I32).rearrange(
                     "p (s w) -> p s w", w=2)[:, :, 1:2], 0)
-        zero_raw(nc.gpsimd, 2)
-        zero_x(nc.gpsimd, 0)
-        for k in range(3, NRAW):
-            zero_raw(nc.gpsimd, k)
-        zero_x(nc.gpsimd, 1)
+        nc.vector.tensor_copy(out=sel[:], in_=ident[:, 0:H].unsqueeze(2).to_broadcast([P, H, E // H]))
+        for k in range(1, NRAW):
+            zero_raw(nc.vector, k)
 
         nc.sync.dma_start(out=mb[0:H, :], in_=mix_b)
         for h in range(HC):
             load_w(0, h, h + 1)
         load_w(1)
         load_w(2)
-        load_x(0)
+        load_x(0, (0, 576))
         load_w(3)
+        load_x(0, (576, E))
         load_w(4)
         load_w(5)
         load_ow(0)
@@ -281,10 +279,11 @@ def tile_mixerblock_pa_kernel(tc, x_proj, mix_mat, mix_b, out_w, out_b, out):
                     nc.vector.tensor_scalar(out=ot, in0=acc[:], scalar1=outb[:, ob:ob + 1], scalar2=None, op0=ALU.add)
                 else:
                     nc.scalar.activation(out=ot, in_=acc[:], func=ACT.Identity, bias=outb[:, ob:ob + 1], scale=1.0)
-                if ob % 2 == 1:
+                first = ob if b == B - 1 and ob >= OB - 2 else ob - 1
+                if ob % 2 == 1 or first == ob:
                     nc.sync.dma_start(
-                        out=out[b].rearrange("(p ob) s -> p ob s", ob=OB)[:, ob - 1:ob + 1, :],
-                        in_=ot_of[0][:, ob % 4 - 1:ob % 4 + 1, :],
+                        out=out[b].rearrange("(p ob) s -> p ob s", ob=OB)[:, first:ob + 1, :],
+                        in_=ot_of[0][:, first % 4:ob % 4 + 1, :],
                     )
 
         v, s = nc.vector.tensor_copy, nc.scalar.copy
@@ -292,6 +291,10 @@ def tile_mixerblock_pa_kernel(tc, x_proj, mix_mat, mix_b, out_w, out_b, out):
         spread_b(s, 1, 0)
         w_mask(0, 0, 1)
         w_regroup_s(0)
+        spread_b(s, 0, 1)
+        spread_b(s, 1, 1)
+        zero_x(nc.vector, 0)
+        zero_x(nc.vector, 1)
         w_mask(0, 1, 2)
         w_regroup_v(1)
         w_mask(1)
@@ -314,8 +317,6 @@ def tile_mixerblock_pa_kernel(tc, x_proj, mix_mat, mix_b, out_w, out_b, out):
         w_regroup_v(6)
         x_quant(0, 0)
         x_regroup(0, 1)
-        spread_b(s, 0, 1)
-        spread_b(s, 1, 1)
         load_x(1)
         load_ow(1)
         w_quant(6)
@@ -325,26 +326,26 @@ def tile_mixerblock_pa_kernel(tc, x_proj, mix_mat, mix_b, out_w, out_b, out):
         mix_mm(0, 0)
         w_regroup_s(9)
         x_quant(0, 1)
-        w_quant(8)
         w_mask(5)
+        w_quant(8)
         mix_exit(0, 0, (0, 1))
         w_regroup_s(11)
         w_quant(9)
         w_regroup_v(10)
+        w_mask(6)
         mix_exit(0, 0, (2, 3))
         for obp in range(2):
             for g in range(2):
                 ow_transpose(obp, g)
         load_x(2)
-        w_mask(6)
         w_quant(10)
         w_quant(11)
         ow_exit(0, 0)
         ow_exit(1, 0)
+        w_mask(7)
         w_regroup_v(12)
         mix_quant(0, 0)
         w_regroup_s(13)
-        w_mask(7)
         ow_exit(0, 1)
         ow_exit(1, 1)
         ow_quant(0, 0)

from contextlib import ExitStack

import concourse.mybir as mybir
from concourse.masks import make_identity

BF16 = mybir.dt.bfloat16
F32 = mybir.dt.float32
U32 = mybir.dt.uint32
U8 = mybir.dt.uint8
I32 = mybir.dt.int32
FP8X4 = mybir.dt.float8_e4m3fn_x4
ALU = mybir.AluOpType
ACT = mybir.ActivationFunctionType

P = 128
B, S, E, H = 4, 512, 1024, 16
FLOPS = 2 * B * E * S * S + 2 * B * S * E * E
HC = 2
NCK = H // HC
NRAW = 6
SLOT = HC * S
PAIRW = 192
HALF = 256
OB = E // P


def regroup(eng_copy, dst, src):
    eng_copy(
        out=dst.rearrange("p (c i) t -> p c t i", i=4),
        in_=src.rearrange("p t (c i) -> p c t i", i=4),
    )


def tile_mixerblock_pa_kernel(tc, x_proj, mix_mat, mix_b, out_w, out_b, out):
    nc = tc.nc
    with ExitStack() as ctx:
        keep = ctx.enter_context(tc.tile_pool(name="keep", bufs=1))
        rot = ctx.enter_context(tc.tile_pool(name="rot", bufs=5))
        xcp = ctx.enter_context(tc.tile_pool(name="xcp", bufs=2))
        xgp = ctx.enter_context(tc.tile_pool(name="xgp", bufs=2))
        ogp = ctx.enter_context(tc.tile_pool(name="ogp", bufs=2))
        mgp = ctx.enter_context(tc.tile_pool(name="mgp", bufs=3))
        mcp = ctx.enter_context(tc.tile_pool(name="mcp", bufs=2))
        ps1p = ctx.enter_context(tc.psum_pool(name="ps1p", bufs=4))
        ps2p = ctx.enter_context(tc.psum_pool(name="ps2p", bufs=4))
        ctx.enter_context(tc.manual_schedule())

        xraw = {}
        owraw = {}
        xc = [keep.tile([P, 8 * PAIRW], U32, name="xc%d" % b, align_bytes=64) for b in range(2)]
        xs = [keep.tile([P, 8 * PAIRW], U8, name="xs%d" % b, align_bytes=64) for b in range(2)]
        raw = [keep.tile([P, 4 * (SLOT + P)], BF16, name="raw%d" % k) for k in range(NRAW)]
        gt = [keep.tile([P, S, 4], BF16, name="gt%d" % k, align_bytes=64) for k in range(4)]
        wc = keep.tile([P, H * S], U32, name="wc", align_bytes=64)
        ws = keep.tile([P, H * S], U8, name="ws", align_bytes=64)
        oc = keep.tile([P, 2, E], U32, name="oc", align_bytes=64)
        osc = keep.tile([P, 2, E], U8, name="osc", align_bytes=64)
        bT = keep.tile([P, 2, S, 4], BF16, name="bT")
        mb = keep.tile([P, S], BF16, name="mb")
        sel = keep.tile([P, H, E // H], BF16, name="sel")
        ident = keep.tile([P, P], BF16, name="ident")
        mask = keep.tile([P, P], BF16, name="mask")
        outb16 = keep.tile([P, OB], BF16, name="outb16")
        outb = keep.tile([P, OB], F32, name="outb")

        def load_x(b, cols=(0, E)):
            if b not in xraw:
                xraw[b] = rot.tile([P, 4, E], BF16, name="xraw", tag="rot")
            lo, hi = cols
            nc.sync.dma_start(
                out=xraw[b][:, :, lo:hi], in_=x_proj[b][:, lo:hi].rearrange("(j p) c -> p j c", p=P))

        def load_ow(q):
            owraw[q] = rot.tile([P, 4, E], BF16, name="owraw", tag="rot")
            nc.sync.dma_start(
                out=owraw[q][:], in_=out_w.rearrange("(p ob) c -> p ob c", ob=OB)[:, 4 * q:4 * q + 4, :])

        def slots(k):
            return raw[k % NRAW][:, 0:4 * SLOT].rearrange("p (j h s) -> p j h s", h=HC, s=S)

        def load_w(k, h0=0, h1=HC):
            for j in range(4):
                nc.sync.dma_start(
                    out=slots(k)[:, j, h0:h1, P * j:S],
                    in_=mix_mat[HC * k + h0:HC * k + h1, P * j:P * (j + 1), P * j:S].rearrange("h p s -> p h s"),
                )

        make_identity(nc, ident[:])
        nc.gpsimd.memset(mask[:], 1.0)
        nc.gpsimd.affine_select(
            out=mask[:], in_=mask[:], pattern=[[1, P]], compare_op=ALU.is_ge,
            fill=0.0, base=0, channel_multiplier=-1,
        )

        def zero_raw(eng, k):
            for j in (1, 3):
                eng.memset(slots(k)[:, j, :, P * (j - 1):P * j].bitcast(I32), 0)

        def zero_x(eng, b):
            eng.memset(
                xc[b][:].bitcast(I32).rearrange("p (i w) -> p i w", w=PAIRW)[:, :, 64:128], 0)
            eng.memset(
                xs[b][:].bitcast(I32).rearrange("p (i w) -> p i w", w=PAIRW // 4)[:, :, 16:32], 0)

        nc.vector.memset(mb[:].bitcast(I32), 0)
        zero_raw(nc.vector, 0)
        for k in range(4):
            nc.vector.memset(
                gt[k][:, 0:HALF, :].rearrange("p s t -> p (s t)").bitcast(I32).rearrange(
                    "p (s w) -> p s w", w=2)[:, :, 1:2], 0)
        nc.vector.tensor_copy(out=sel[:], in_=ident[:, 0:H].unsqueeze(2).to_broadcast([P, H, E // H]))
        for k in range(1, NRAW):
            zero_raw(nc.vector, k)

        nc.sync.dma_start(out=mb[0:H, :], in_=mix_b)
        for h in range(HC):
            load_w(0, h, h + 1)
        load_w(1)
        load_w(2)
        load_x(0, (0, 576))
        load_w(3)
        load_x(0, (576, E))
        load_w(4)
        load_w(5)
        load_ow(0)
        nc.sync.dma_start(out=outb16[:], in_=out_b.rearrange("(p ob) -> p ob", ob=OB))

        def spread_b(eng_copy, half, g):
            pb = ps2p.tile([P, 4, HALF], BF16, name="pb", tag="ps2")
            for j in range(4):
                i = 4 * g + j
                nc.tensor.matmul(
                    pb[:, j, :], lhsT=sel[:, 2 * i:2 * i + 2, :].rearrange("p h e -> p (h e)"),
                    rhs=mb[:, HALF * half:HALF * (half + 1)], start=True, stop=True)
            eng_copy(out=bT[:, g, HALF * half:HALF * (half + 1), :], in_=pb[:].rearrange("p j s -> p s j"))

        xg_of = {}
        XCUT = (0, 576, 1024)

        def x_regroup(b, ch):
            lo, hi = XCUT[ch], XCUT[ch + 1]
            xg = xgp.tile([P, 576, 4], BF16, name="xg", align_bytes=64)
            xg_of[(b, ch)] = xg
            regroup(nc.scalar.copy, xg[:, 0:hi - lo, :], xraw[b][:, :, lo:hi])

        def x_quant(b, ch):
            lo, hi = XCUT[ch], XCUT[ch + 1]
            flat = xg_of[(b, ch)][:].rearrange("p c t -> p (c t)")
            c0 = lo
            while c0 < hi:
                c1 = min(c0 + P if c0 % P else c0 + 64, hi)
                w0 = PAIRW * (c0 // P) + (P if c0 % P else 0)
                nc.vector.quantize_mx(
                    out=xc[b % 2][:, w0:w0 + c1 - c0].bitcast(FP8X4),
                    scales=xs[b % 2][:, w0:w0 + c1 - c0],
                    in_=flat[:, 4 * (c0 - lo):4 * (c1 - lo)],
                )
                c0 = c1

        def w_mask(k, h0=0, h1=HC):
            d = raw[k % NRAW][:].rearrange("p (j x) -> p j x", x=SLOT + P)
            d = d[:, :, 0:SLOT].rearrange("p j (h s) -> p j h s", s=S)[:, :, h0:h1, 0:P]
            nc.vector.tensor_tensor(
                out=d, in0=d, in1=mask[:].unsqueeze(1).unsqueeze(1).to_broadcast([P, 4, h1 - h0, P]), op=ALU.mult)

        g_of = {}

        done = {0: 0, 1: 0}

        def w_regroup(h, who):
            g = gt[2 * who + done[who] % 2]
            done[who] += 1
            g_of[h] = g
            eng_copy = (nc.vector.tensor_copy, nc.scalar.copy)[who]
            regroup(eng_copy, g[:, 0:HALF, 0:2], slots(h // HC)[:, 0:2, h % HC, 0:HALF])
            regroup(eng_copy, g[:, HALF:S, :], slots(h // HC)[:, :, h % HC, HALF:S])

        def w_regroup_v(h):
            w_regroup(h, 0)

        def w_regroup_s(h):
            w_regroup(h, 1)

        def w_quant(h):
            nc.vector.quantize_mx(
                out=wc[:, h * S:(h + 1) * S].bitcast(FP8X4),
                scales=ws[:, h * S:(h + 1) * S],
                in_=g_of[h][:].rearrange("p s t -> p (s t)"),
            )

        pt_of = {}
        og_of = {}

        def ow_transpose(obp, g):
            pt = ps2p.tile([P, 2, 4, P], BF16, name="pt", tag="ps2")
            pt_of[(obp, g)] = pt
            for u in range(2):
                for j in range(4):
                    c0 = 512 * g + P * j
                    nc.tensor.transpose(pt[:, u, j, :], owraw[obp // 2][:, 2 * (obp % 2) + u, c0:c0 + P], ident[:])

        def ow_exit(obp, g):
            if obp % 2 == 0:
                og_of[(obp // 2, g)] = ogp.tile([P, 4, P, 4], BF16, name="og", align_bytes=64)
            u0 = 2 * (obp % 2)
            nc.scalar.copy(out=og_of[(obp // 2, g)][:, u0:u0 + 2, :, :], in_=pt_of[(obp, g)][:].rearrange("p u j o -> p u o j"))

        def ow_quant(q, g):
            nc.vector.quantize_mx(
                out=oc[:, g, 4 * P * q:4 * P * (q + 1)].bitcast(FP8X4),
                scales=osc[:, g, 4 * P * q:4 * P * (q + 1)],
                in_=og_of[(q, g)][:].rearrange("p u o j -> p (u o j)"),
            )

        acc1_of = {}
        mg_of = {}
        mc_of = {}
        ms_of = {}

        def mix_mm(b, g):
            for q in range(4):
                acc = ps1p.tile([P, 4, P], F32, name="acc1")
                acc1_of[(b, g, q)] = acc
                for j in range(4):
                    i = 4 * g + j
                    for h2 in range(2):
                        x0 = PAIRW * i + 64 * h2
                        w0 = (2 * i + h2) * S + P * q
                        nc.tensor.matmul_mx(
                            out=acc[:, j, :],
                            lhsT=xc[b % 2][:, x0:x0 + P].bitcast(FP8X4),
                            lhsT_scale=xs[b % 2][:, x0:x0 + P],
                            rhs=wc[:, w0:w0 + P].bitcast(FP8X4),
                            rhs_scale=ws[:, w0:w0 + P],
                            start=(h2 == 0),
                            stop=(h2 == 1),
                        )

        def mix_exit(b, g, qs=range(4)):
            for q in qs:
                if q == 0:
                    mg_of[(b, g)] = mgp.tile([P, S, 4], BF16, name="mg", align_bytes=64)
                nc.vector.tensor_tensor(
                    out=mg_of[(b, g)][:, P * q:P * (q + 1), :],
                    in0=acc1_of[(b, g, q)][:].rearrange("p j s -> p s j"),
                    in1=bT[:, g, P * q:P * (q + 1), :],
                    op=ALU.add,
                )

        def mix_quant(b, g):
            if g == 0:
                mc_of[b] = mcp.tile([P, 2, S], U32, name="mc", align_bytes=64)
                ms_of[b] = mcp.tile([P, 2, S], U8, name="ms", align_bytes=64)
            nc.vector.quantize_mx(
                out=mc_of[b][:, g, :].bitcast(FP8X4),
                scales=ms_of[b][:, g, :],
                in_=mg_of[(b, g)][:].rearrange("p s j -> p (s j)"),
            )

        ot_of = {}

        def project(b, obs, on_vector=()):
            for ob in obs:
                acc = ps2p.tile([P, S], F32, name="acc2", tag="ps2")
                for g in range(2):
                    nc.tensor.matmul_mx(
                        out=acc[:],
                        lhsT=oc[:, g, P * ob:P * (ob + 1)].bitcast(FP8X4),
                        lhsT_scale=osc[:, g, P * ob:P * (ob + 1)],
                        rhs=mc_of[b][:, g, :].bitcast(FP8X4),
                        rhs_scale=ms_of[b][:, g, :],
                        start=(g == 0),
                        stop=(g == 1),
                    )
                if ob % 4 == 0:
                    ot_of[0] = rot.tile([P, 4, S], F32, name="ot4", tag="rot")
                ot = ot_of[0][:, ob % 4, :]
                if ob in on_vector:
                    nc.vector.tensor_scalar(out=ot, in0=acc[:], scalar1=outb[:, ob:ob + 1], scalar2=None, op0=ALU.add)
                else:
                    nc.scalar.activation(out=ot, in_=acc[:], func=ACT.Identity, bias=outb[:, ob:ob + 1], scale=1.0)
                first = ob if b == B - 1 and ob >= OB - 2 else ob - 1
                if ob % 2 == 1 or first == ob:
                    nc.sync.dma_start(
                        out=out[b].rearrange("(p ob) s -> p ob s", ob=OB)[:, first:ob + 1, :],
                        in_=ot_of[0][:, first % 4:ob % 4 + 1, :],
                    )

        v, s = nc.vector.tensor_copy, nc.scalar.copy
        spread_b(s, 0, 0)
        spread_b(s, 1, 0)
        w_mask(0, 0, 1)
        w_regroup_s(0)
        spread_b(s, 0, 1)
        spread_b(s, 1, 1)
        zero_x(nc.vector, 0)
        zero_x(nc.vector, 1)
        w_mask(0, 1, 2)
        w_regroup_v(1)
        w_mask(1)
        w_quant(0)
        w_regroup_s(3)
        w_regroup_v(2)
        w_quant(1)
        load_w(6)
        w_mask(2)
        w_regroup_s(5)
        w_quant(2)
        w_quant(3)
        w_regroup_v(4)
        load_w(7)
        x_regroup(0, 0)
        w_mask(3)
        w_regroup_s(7)
        w_quant(5)
        w_quant(4)
        w_regroup_v(6)
        x_quant(0, 0)
        x_regroup(0, 1)
        load_x(1)
        load_ow(1)
        w_quant(6)
        w_mask(4)
        w_quant(7)
        w_regroup_v(8)
        mix_mm(0, 0)
        w_regroup_s(9)
        x_quant(0, 1)
        w_mask(5)
        w_quant(8)
        mix_exit(0, 0, (0, 1))
        w_regroup_s(11)
        w_quant(9)
        w_regroup_v(10)
        w_mask(6)
        mix_exit(0, 0, (2, 3))
        for obp in range(2):
            for g in range(2):
                ow_transpose(obp, g)
        load_x(2)
        w_quant(10)
        w_quant(11)
        ow_exit(0, 0)
        ow_exit(1, 0)
        w_mask(7)
        w_regroup_v(12)
        mix_quant(0, 0)
        w_regroup_s(13)
        ow_exit(0, 1)
        ow_exit(1, 1)
        ow_quant(0, 0)
        w_regroup_v(14)
        w_quant(12)
        w_regroup_s(15)
        w_quant(13)
        ow_quant(0, 1)
        w_quant(14)
        x_regroup(1, 0)
        for obp in range(2, 4):
            for g in range(2):
                ow_transpose(obp, g)
        ow_exit(2, 0)
        ow_exit(3, 0)
        w_quant(15)
        mix_mm(0, 1)
        ow_exit(2, 1)
        ow_exit(3, 1)
        x_quant(1, 0)
        ow_quant(1, 0)
        nc.vector.tensor_copy(out=outb[:], in_=outb16[:])
        mix_exit(0, 1, (0, 1))
        x_regroup(1, 1)
        ow_quant(1, 1)
        mix_exit(0, 1, (2, 3))
        mix_mm(1, 0)
        x_quant(1, 1)
        mix_quant(0, 1)
        x_regroup(2, 0)
        load_x(3)
        for b in range(1, B):
            project(b - 1, range(4))
            mix_exit(b, 0)
            mix_mm(b, 1)
            if b + 1 < B:
                x_quant(b + 1, 0)
            if b + 1 < B:
                x_regroup(b + 1, 1)
            project(b - 1, range(4, 8))
            mix_quant(b, 0)
            mix_exit(b, 1)
            if b + 1 < B:
                mix_mm(b + 1, 0)
                x_quant(b + 1, 1)
            if b + 2 < B:
                x_regroup(b + 2, 0)
            mix_quant(b, 1)
        project(B - 1, range(OB), (0, 2, 4, 6))
